import numpy as np
import ml_dtypes


def mxq(x, axis, fmt="e4m3"):
    dtype, down = {"e4m3": (ml_dtypes.float8_e4m3fn, 7), "e5m2": (ml_dtypes.float8_e5m2, 14)}[fmt]
    v = np.moveaxis(np.asarray(x, np.float32).astype(ml_dtypes.bfloat16).astype(np.float64), axis, -1)
    blocks = v.reshape(v.shape[:-1] + (-1, 32))
    amax = np.abs(blocks).max(-1, keepdims=True)
    byte = np.maximum(np.where(amax > 0, np.frexp(amax)[1] - 1 + 127, 0) - down, 1)
    scale = np.exp2(byte - 127.0)
    codes = (blocks / scale).astype(np.float32).astype(dtype).astype(np.float64)
    return np.moveaxis((codes * scale).reshape(v.shape), -1, axis)


WIDE = False


def mx_kscale(k):
    if not WIDE:
        return np.ones(k)
    levels = np.array([10, -10, 5, -5, 0])
    a = np.random.permutation(np.resize(levels, k // 512 * 4)).reshape(k // 512, 4)
    idx = np.arange(k)
    return np.exp2(a[idx // 512, idx % 128 // 32])


BF16 = ml_dtypes.bfloat16


def bf(x):
    return np.asarray(x, np.float32).astype(BF16)


def f64(x):
    return np.asarray(x).astype(np.float64)


E2M1 = np.array([0.0, 0.5, 1.0, 1.5, 2.0, 3.0, 4.0, 6.0, -0.0, -0.5, -1.0, -1.5, -2.0, -3.0, -4.0, -6.0])


def pack_weight(w, fmt):
    k, n = w.shape
    w = f64(bf(w)).reshape(k // 32, 32, n)
    amax = np.abs(w).max(1)
    if fmt == "e4m3":
        byte = np.frexp(amax)[1] - 1 + 127 - 7
    else:
        mant, ex = np.frexp(amax / 6.0)
        byte = np.where(mant > 0.5, ex, ex - 1) + 127
    byte = np.clip(np.where(amax > 0, byte, 1), 1, 254)
    scaled = (w * np.exp2(127.0 - byte)[:, None, :]).reshape(k, n).astype(np.float32)
    by_word = np.ascontiguousarray(scaled.reshape(k // 512, 128, 4, n).transpose(0, 1, 3, 2))
    if fmt == "e4m3":
        words = by_word.astype(ml_dtypes.float8_e4m3fn).view(np.uint8)
    else:
        c = by_word.astype(ml_dtypes.float4_e2m1fn).view(np.uint8) & 0xF
        words = c[..., 0::2] | (c[..., 1::2] << 4)
    return np.ascontiguousarray(words), np.ascontiguousarray(byte.astype(np.uint8).reshape(k // 512, 16, n))


def unpack_weight(words, scales, fmt):
    g, p, n, _ = words.shape
    if fmt == "e4m3":
        vals = np.ascontiguousarray(words).view(ml_dtypes.float8_e4m3fn).astype(np.float64)
    else:
        nib = np.empty((g, p, n, 4), np.uint8)
        nib[..., 0::2] = words & 0xF
        nib[..., 1::2] = words >> 4
        vals = E2M1[nib]
    vals = vals * np.repeat(np.exp2(scales.astype(np.float64) - 127.0), 8, axis=1)[..., None]
    return vals.transpose(0, 1, 3, 2).reshape(g * 512, n)

def pack4(w):
    words, scales = pack_weight(w, "e2m1")
    return words.reshape(words.shape[0], 128, -1), scales


def unpack4(words, scales):
    return unpack_weight(words.reshape(words.shape[0], 128, -1, 2), scales, "e2m1")


B, T, C, NH, NKV, HS = 2, 256, 2048, 16, 4, 128
EPS = 1e-6
ROPE_THETA = 10000.0
HALF = HS // 2
KW = NKV * HS


def rmsnorm(u, gain):
    ms = np.mean(np.square(u), axis=-1, keepdims=True)
    return u * (1.0 / np.sqrt(ms + EPS)) * gain


def rope_cos_sin():
    inv_freq = ROPE_THETA ** (-np.arange(0, HS, 2, dtype=np.float64) / HS)
    ang = np.arange(T, dtype=np.float64)[:, None] * inv_freq[None, :]
    return np.cos(ang), np.sin(ang)


def apply_rope(u, cos, sin):
    u1, u2 = u[..., :HALF], u[..., HALF:]
    c = cos[None, :, None, :]
    s = sin[None, :, None, :]
    return np.concatenate([u1 * c - u2 * s, u1 * s + u2 * c], axis=-1)


def setup_inputs():
    s = mx_kscale(C)
    x = bf(np.random.standard_normal((B, T, C)) * s)
    Wq_words, Wq_scales = pack4(np.random.standard_normal((C, NH * HS)) / np.sqrt(C) / s[:, None])
    Wkv_words, Wkv_scales = pack4(np.random.standard_normal((C, 2 * KW)) / np.sqrt(C) / s[:, None])
    return {
        "x": x,
        "Wq_words": Wq_words,
        "Wq_scales": Wq_scales,
        "Wkv_words": Wkv_words,
        "Wkv_scales": Wkv_scales,
        "q_scale": bf(1.0 + 0.1 * np.random.standard_normal(HS)),
        "k_scale": bf(1.0 + 0.1 * np.random.standard_normal(HS)),
        "v1": bf(np.random.standard_normal((B, T, NKV, HS))),
        "value_lambda": bf(np.random.uniform(0.2, 0.7, (1,))),
    }


def reference(x, Wq_words, Wq_scales, Wkv_words, Wkv_scales, q_scale, k_scale, v1, value_lambda):
    xq = mxq(f64(x), 2, "e4m3")
    q = (xq @ unpack4(Wq_words, Wq_scales)).reshape(B, T, NH, HS)
    kv = xq @ unpack4(Wkv_words, Wkv_scales)
    k = kv[..., :KW].reshape(B, T, NKV, HS)
    v = kv[..., KW:].reshape(B, T, NKV, HS)
    lam = f64(value_lambda).reshape(())
    v = v + (1.0 - lam) * f64(v1)
    q = rmsnorm(q, f64(q_scale))
    k = rmsnorm(k, f64(k_scale))
    cos, sin = rope_cos_sin()
    return apply_rope(q, cos, sin), apply_rope(k, cos, sin), v

@@ -1,0 +1,266 @@
+import math
+
+import concourse.mybir as mybir
+from concourse.masks import make_identity
+
+F32 = mybir.dt.float32
+BF16 = mybir.dt.bfloat16
+I32 = mybir.dt.int32
+U32 = mybir.dt.uint32
+U8 = mybir.dt.uint8
+FP8X4 = mybir.dt.float8_e4m3fn_x4
+FP4X4 = mybir.dt.float4_e2m1fn_x4
+ALU = mybir.AluOpType
+ACT = mybir.ActivationFunctionType
+
+P = 128
+BATCH, T, C = 2, 256, 2048
+HEAD = 128
+HALF = HEAD // 2
+DOUBLINGS = 6
+K_PASS = 512
+PASSES = C // K_PASS
+BANK = 512
+HEADS_PER_BANK = BANK // HEAD
+TILES_PER_BATCH = T // P
+TOKEN_TILES = BATCH * TILES_PER_BATCH
+CHUNK = 2 * BANK
+Q_GROUPS, K_GROUP, V_GROUP = 4, 4, 5
+EPS = 1e-6
+ROPE_THETA = 10000.0
+ROUND_MAGIC = 1.5 * 2.0**23
+
+FLOPS = 2 * BATCH * T * C * (Q_GROUPS + 2) * BANK
+
+
+def tile_attention_pa_kernel(
+    tc, x, Wq_words, Wq_scales, Wkv_words, Wkv_scales, q_scale, k_scale, v1, value_lambda,
+    out_0, out_1, out_2,
+):
+    nc = tc.nc
+    x_rows = x.flatten_outer_dims()
+    v1_rows = v1.rearrange("b t h d -> (b t) (h d)")
+    q_rows = out_0.rearrange("b t h d -> (b t) (h d)")
+    k_rows = out_1.rearrange("b t h d -> (b t) (h d)")
+    v_rows = out_2.rearrange("b t h d -> (b t) (h d)")
+
+    with tc.tile_pool(name="keep", bufs=1) as keep, \
+            tc.tile_pool(name="stage", bufs=2) as stage, \
+            tc.tile_pool(name="small", bufs=4) as small, \
+            tc.tile_pool(name="work", bufs=4) as work, \
+            tc.tile_pool(name="results", bufs=8) as results, \
+            tc.psum_pool(name="psum_t", bufs=2) as psum_t, \
+            tc.psum_pool(name="psum_o", bufs=6) as psum_o, \
+            tc.manual_schedule():
+
+        x_sb = [keep.tile([P, C], BF16, name="x_sb%d" % m) for m in range(TOKEN_TILES)]
+        x_codes = [
+            keep.tile([P, PASSES, P], U32, name="x_codes%d" % m, align_bytes=64)
+            for m in range(TOKEN_TILES)
+        ]
+        x_scales = [
+            keep.tile([P, PASSES, P], U8, name="x_scales%d" % m, align_bytes=64)
+            for m in range(TOKEN_TILES)
+        ]
+        w_words = [
+            keep.tile([P, PASSES, 2 * CHUNK], U8, name="w_words%d" % c, align_bytes=64)
+            for c in range(3)
+        ]
+        w_planes = [
+            keep.tile([P, PASSES, CHUNK], U8, name="w_planes%d" % c, align_bytes=64)
+            for c in range(3)
+        ]
+        v1_sb = keep.tile([P, TOKEN_TILES, BANK], BF16)
+        gain_q = keep.tile([P, HEAD], BF16)
+        gain_k = keep.tile([P, HEAD], BF16)
+        lam = keep.tile([P, 1], BF16)
+        identity = keep.tile([P, P], F32)
+        eps = keep.tile([P, 1], F32)
+        warm = keep.tile([P, 1], F32)
+        squares = keep.tile([P, HEAD], F32)
+
+        def load_x(m):
+            nc.sync.dma_start(out=x_sb[m][:], in_=x_rows[m * P:(m + 1) * P, :])
+
+        def load_weights(c, words, scales, first_column):
+            nc.vector.memset(w_planes[c][:].bitcast(I32), 0)
+            scale_words = scales.bitcast(I32)[:, :, first_column // 4:(first_column + CHUNK) // 4]
+            for row in range(8):
+                partition = 32 * (row // 4) + row % 4
+                nc.sync.dma_start(
+                    out=w_planes[c][partition:P:64, :, :].bitcast(I32),
+                    in_=scale_words[:, row:16:8, :].rearrange("g q w -> q g w"),
+                )
+            nc.sync.dma_start(
+                out=w_words[c][:].bitcast(I32),
+                in_=words.bitcast(I32)[:, :, first_column // 2:(first_column + CHUNK) // 2]
+                .rearrange("g p w -> p g w"),
+            )
+
+        nc.vector.memset(eps[:], EPS)
+        nc.scalar.dma_start(out=gain_q[:], in_=q_scale.partition_broadcast(P))
+        nc.scalar.dma_start(out=gain_k[:], in_=k_scale.partition_broadcast(P))
+        nc.scalar.dma_start(out=lam[:], in_=value_lambda.partition_broadcast(P))
+        nc.scalar.activation(out=warm[:], in_=eps[:], func=ACT.Sin)
+
+        make_identity(nc, identity[:])
+        position_i = keep.tile([P, TILES_PER_BATCH], I32)
+        nc.gpsimd.iota(position_i[:], pattern=[[P, TILES_PER_BATCH]], base=0, channel_multiplier=1)
+
+        load_x(0)
+        load_x(1)
+        load_weights(0, Wq_words, Wq_scales, 0)
+
+        freq = keep.tile([P, 4, HALF], F32)
+        nc.vector.memset(freq[:, :, 0:1], 1.0)
+        nc.vector.memset(freq[:, 1:2, 0:1], -1.0)
+        for doubling in range(DOUBLINGS):
+            step = 2 ** doubling
+            nc.vector.tensor_scalar_mul(
+                out=freq[:, :, step:2 * step], in0=freq[:, :, 0:step],
+                scalar1=ROPE_THETA ** (-step / HALF),
+            )
+        position = keep.tile([P, TILES_PER_BATCH], F32)
+        nc.vector.tensor_copy(out=position[:], in_=position_i[:])
+        angle = keep.tile([P, TILES_PER_BATCH, 4, HALF], F32)
+        for a in range(TILES_PER_BATCH):
+            nc.vector.tensor_scalar_mul(out=angle[:, a, :, :], in0=freq[:], scalar1=position[:, a:a + 1])
+        nc.vector.tensor_scalar_add(
+            out=angle[:, :, 0:4:3, :], in0=angle[:, :, 0:4:3, :], scalar1=math.pi / 2
+        )
+        angle_flat = angle[:].rearrange("p a b i -> p (a b i)")
+        turns = keep.tile([P, TILES_PER_BATCH * 4 * HALF], F32)
+        nc.vector.tensor_scalar(
+            out=turns[:], in0=angle_flat, scalar1=1.0 / (2.0 * math.pi), scalar2=ROUND_MAGIC,
+            op0=ALU.mult, op1=ALU.add,
+        )
+        nc.vector.tensor_scalar(
+            out=turns[:], in0=turns[:], scalar1=ROUND_MAGIC, scalar2=-2.0 * math.pi,
+            op0=ALU.subtract, op1=ALU.mult,
+        )
+        nc.vector.tensor_tensor(out=angle_flat, in0=angle_flat, in1=turns[:], op=ALU.add)
+        trig = keep.tile([P, TILES_PER_BATCH * 2, HEAD], F32)
+        nc.scalar.activation(
+            out=trig[:].rearrange("p c j -> p (c j)"), in_=angle_flat, func=ACT.Sin
+        )
+
+        load_weights(1, Wq_words, Wq_scales, CHUNK)
+        load_weights(2, Wkv_words, Wkv_scales, 0)
+        load_x(2)
+        load_x(3)
+        nc.sync.dma_start(out=v1_sb[:], in_=v1_rows.rearrange("(m p) c -> p m c", p=P))
+
+        def rope_table(gain, name):
+            table = keep.tile([P, TILES_PER_BATCH * 2, HEAD], F32, name=name)
+            nc.vector.tensor_tensor(
+                out=table[:], in0=trig[:],
+                in1=gain[:].unsqueeze(1).to_broadcast([P, TILES_PER_BATCH * 2, HEAD]),
+                op=ALU.mult,
+            )
+            return table
+
+        table_q = rope_table(gain_q, "table_q")
+        table_k = rope_table(gain_k, "table_k")
+        one_minus_lambda = keep.tile([P, 1], F32)
+        nc.vector.tensor_scalar(
+            out=one_minus_lambda[:], in0=lam[:], scalar1=-1.0, scalar2=1.0,
+            op0=ALU.mult, op1=ALU.add,
+        )
+
+        def quantise_token_tile(m):
+            x_words = x_sb[m][:].bitcast(F32)
+            grouped = stage.tile([P, PASSES, P, 4], BF16, align_bytes=64)
+            grouped_words = grouped[:].bitcast(F32)
+            for pair in range(PASSES // 2):
+                turned = psum_t.tile([P, 2, 2, P], F32)
+                for j in range(2):
+                    first_word = (K_PASS // 2) * (2 * pair + j)
+                    for u in range(2):
+                        nc.tensor.transpose(
+                            turned[:, j, u, :],
+                            x_words[:, first_word + u:first_word + K_PASS // 2:2],
+                            identity[:],
+                        )
+                nc.scalar.copy(
+                    out=grouped_words[:, 2 * pair:2 * pair + 2, :, :],
+                    in_=turned[:].rearrange("p j u r -> p j r u"),
+                )
+            nc.vector.quantize_mx(
+                out=x_codes[m][:].rearrange("p g r -> p (g r)").bitcast(FP8X4),
+                scales=x_scales[m][:].rearrange("p g r -> p (g r)"),
+                in_=grouped[:].rearrange("p g r t -> p (g r t)"),
+            )
+
+        def mix_values(acc, m, result):
+            nc.vector.scalar_tensor_tensor(
+                out=result[:], in0=v1_sb[:, m, :], scalar=one_minus_lambda[:, 0:1],
+                in1=acc[:], op0=ALU.mult, op1=ALU.add,
+            )
+
+        def norm_and_rope(acc, a, table, result):
+            sum_squares = small.tile([P, HEADS_PER_BANK], F32)
+            for h in range(HEADS_PER_BANK):
+                nc.scalar.activation(
+                    out=squares[:], in_=acc[:, h * HEAD:(h + 1) * HEAD], func=ACT.Square,
+                    accum_out=sum_squares[:, h:h + 1],
+                )
+            rms = small.tile([P, HEADS_PER_BANK], F32)
+            nc.scalar.activation(
+                out=rms[:], in_=sum_squares[:], func=ACT.Sqrt, bias=eps[:, 0:1], scale=1.0 / HEAD
+            )
+            rstd = small.tile([P, HEADS_PER_BANK], F32)
+            nc.vector.reciprocal(out=rstd[:], in_=rms[:])
+            products = work.tile([P, HEADS_PER_BANK, 2, HEAD], F32)
+            for h in range(HEADS_PER_BANK):
+                nc.vector.scalar_tensor_tensor(
+                    out=products[:, h, :, :],
+                    in0=acc[:, h * HEAD:(h + 1) * HEAD].unsqueeze(1).to_broadcast([P, 2, HEAD]),
+                    scalar=rstd[:, h:h + 1],
+                    in1=table[:, 2 * a:2 * a + 2, :],
+                    op0=ALU.mult, op1=ALU.mult,
+                )
+            terms = products[:].rearrange("p h o (s i) -> p (h o) s i", s=2)
+            nc.gpsimd.tensor_tensor(
+                out=result[:].rearrange("p (c i) -> p c i", i=HALF),
+                in0=terms[:, :, 0, :], in1=terms[:, :, 1, :], op=ALU.add,
+            )
+
+        def project(batch, group):
+            chunk, half = group // 2, group % 2
+            for a in range(TILES_PER_BATCH):
+                m = batch * TILES_PER_BATCH + a
+                token_rows = slice(m * P, (m + 1) * P)
+                acc = psum_o.tile([P, BANK], F32)
+                for g in range(PASSES):
+                    nc.tensor.matmul_mx(
+                        out=acc[:],
+                        lhsT=x_codes[m][:, g, :].bitcast(FP8X4),
+                        lhsT_scale=x_scales[m][:, g, :],
+                        rhs=w_words[chunk][:, g, 2 * BANK * half:2 * BANK * (half + 1)].bitcast(FP4X4),
+                        rhs_scale=w_planes[chunk][:, g, BANK * half:BANK * (half + 1)],
+                        start=(g == 0),
+                        stop=(g == PASSES - 1),
+                    )
+                result = results.tile([P, BANK], F32)
+                if group == V_GROUP:
+                    mix_values(acc, m, result)
+                    nc.sync.dma_start(out=v_rows[token_rows, :], in_=result[:])
+                elif group == K_GROUP:
+                    norm_and_rope(acc, a, table_k, result)
+                    nc.sync.dma_start(out=k_rows[token_rows, :], in_=result[:])
+                else:
+                    norm_and_rope(acc, a, table_q, result)
+                    nc.sync.dma_start(
+                        out=q_rows[token_rows, group * BANK:(group + 1) * BANK], in_=result[:]
+                    )
+
+        quantise_token_tile(0)
+        quantise_token_tile(1)
+        nc.scalar.activation(out=warm[:], in_=eps[:], func=ACT.Sqrt)
+        for group in range(V_GROUP):
+            project(0, group)
+        quantise_token_tile(2)
+        quantise_token_tile(3)
+        project(0, V_GROUP)
+        for group in range(V_GROUP + 1):
+            project(1, group)

@@ -28,6 +28,7 @@ CHUNK = 2 * BANK
 Q_GROUPS, K_GROUP, V_GROUP = 4, 4, 5
 EPS = 1e-6
 ROPE_THETA = 10000.0
+SMALL_COLUMNS = 2 * HEAD + 2
 ROUND_MAGIC = 1.5 * 2.0**23
 
 FLOPS = 2 * BATCH * T * C * (Q_GROUPS + 2) * BANK
@@ -71,9 +72,8 @@ def tile_attention_pa_kernel(
             for c in range(3)
         ]
         v1_sb = keep.tile([P, TOKEN_TILES, BANK], BF16)
-        gain_q = keep.tile([P, HEAD], BF16)
-        gain_k = keep.tile([P, HEAD], BF16)
-        lam = keep.tile([P, 1], BF16)
+        small_row = keep.tile([P, SMALL_COLUMNS], BF16)
+        ones = keep.tile([P, P], BF16)
         identity = keep.tile([P, P], F32)
         eps = keep.tile([P, 1], F32)
         warm = keep.tile([P, 1], F32)
@@ -98,9 +98,13 @@ def tile_attention_pa_kernel(
             )
 
         nc.vector.memset(eps[:], EPS)
-        nc.scalar.dma_start(out=gain_q[:], in_=q_scale.partition_broadcast(P))
-        nc.scalar.dma_start(out=gain_k[:], in_=k_scale.partition_broadcast(P))
-        nc.scalar.dma_start(out=lam[:], in_=value_lambda.partition_broadcast(P))
+        nc.vector.memset(small_row[:], 0.0)
+        nc.vector.memset(ones[:], 1.0)
+        nc.scalar.dma_start(out=small_row[0:1, 0:HEAD], in_=q_scale.rearrange("(o n) -> o n", o=1))
+        nc.scalar.dma_start(out=small_row[0:1, HEAD:2 * HEAD], in_=k_scale.rearrange("(o n) -> o n", o=1))
+        nc.scalar.dma_start(
+            out=small_row[0:1, 2 * HEAD:2 * HEAD + 1], in_=value_lambda.rearrange("(o n) -> o n", o=1)
+        )
         nc.scalar.activation(out=warm[:], in_=eps[:], func=ACT.Sin)
 
         make_identity(nc, identity[:])
@@ -150,11 +154,19 @@ def tile_attention_pa_kernel(
         load_x(3)
         nc.sync.dma_start(out=v1_sb[:], in_=v1_rows.rearrange("(m p) c -> p m c", p=P))
 
+        spread = psum_t.tile([P, BANK], F32, tag="turned")
+        nc.tensor.matmul(
+            out=spread[:, 0:SMALL_COLUMNS], lhsT=ones[:], rhs=small_row[:], start=True, stop=True
+        )
+        gain_q = spread[:, 0:HEAD]
+        gain_k = spread[:, HEAD:2 * HEAD]
+        lam = spread[:, 2 * HEAD:2 * HEAD + 1]
+
         def rope_table(gain, name):
             table = keep.tile([P, TILES_PER_BATCH * 2, HEAD], F32, name=name)
             nc.vector.tensor_tensor(
                 out=table[:], in0=trig[:],
-                in1=gain[:].unsqueeze(1).to_broadcast([P, TILES_PER_BATCH * 2, HEAD]),
+                in1=gain.unsqueeze(1).to_broadcast([P, TILES_PER_BATCH * 2, HEAD]),
                 op=ALU.mult,
             )
             return table
@@ -163,7 +175,7 @@ def tile_attention_pa_kernel(
         table_k = rope_table(gain_k, "table_k")
         one_minus_lambda = keep.tile([P, 1], F32)
         nc.vector.tensor_scalar(
-            out=one_minus_lambda[:], in0=lam[:], scalar1=-1.0, scalar2=1.0,
+            out=one_minus_lambda[:], in0=lam, scalar1=-1.0, scalar2=1.0,
             op0=ALU.mult, op1=ALU.add,
         )
 
@@ -172,7 +184,7 @@ def tile_attention_pa_kernel(
             grouped = stage.tile([P, PASSES, P, 4], BF16, align_bytes=64)
             grouped_words = grouped[:].bitcast(F32)
             for pair in range(PASSES // 2):
-                turned = psum_t.tile([P, 2, 2, P], F32)
+                turned = psum_t.tile([P, 2, 2, P], F32, tag="turned")
                 for j in range(2):
                     first_word = (K_PASS // 2) * (2 * pair + j)
                     for u in range(2):

@@ -28,6 +28,7 @@ CHUNK = 2 * BANK
 Q_GROUPS, K_GROUP, V_GROUP = 4, 4, 5
 EPS = 1e-6
 ROPE_THETA = 10000.0
+SQUARE_SLICES = 8
 SMALL_COLUMNS = 2 * HEAD + 2
 ROUND_MAGIC = 1.5 * 2.0**23
 
@@ -77,7 +78,8 @@ def tile_attention_pa_kernel(
         identity = keep.tile([P, P], F32)
         eps = keep.tile([P, 1], F32)
         warm = keep.tile([P, 1], F32)
-        squares = keep.tile([P, HEAD], F32)
+        squares = keep.tile([P, SQUARE_SLICES, HEAD], F32)
+        squares_written = []
 
         def load_x(m):
             nc.sync.dma_start(out=x_sb[m][:], in_=x_rows[m * P:(m + 1) * P, :])
@@ -213,15 +215,16 @@ def tile_attention_pa_kernel(
             sum_squares = small.tile([P, HEADS_PER_BANK], F32)
             for h in range(HEADS_PER_BANK):
                 nc.scalar.activation(
-                    out=squares[:], in_=acc[:, h * HEAD:(h + 1) * HEAD], func=ACT.Square,
+                    out=squares[:, len(squares_written) % SQUARE_SLICES, :],
+                    in_=acc[:, h * HEAD:(h + 1) * HEAD], func=ACT.Square,
                     accum_out=sum_squares[:, h:h + 1],
                 )
-            rms = small.tile([P, HEADS_PER_BANK], F32)
-            nc.scalar.activation(
-                out=rms[:], in_=sum_squares[:], func=ACT.Sqrt, bias=eps[:, 0:1], scale=1.0 / HEAD
-            )
+                squares_written.append(h)
             rstd = small.tile([P, HEADS_PER_BANK], F32)
-            nc.vector.reciprocal(out=rstd[:], in_=rms[:])
+            nc.scalar.activation(
+                out=rstd[:], in_=sum_squares[:], func=ACT.Abs_reciprocal_sqrt,
+                bias=eps[:, 0:1], scale=1.0 / HEAD,
+            )
             products = work.tile([P, HEADS_PER_BANK, 2, HEAD], F32)
             for h in range(HEADS_PER_BANK):
                 nc.vector.scalar_tensor_tensor(
@@ -268,7 +271,7 @@ def tile_attention_pa_kernel(
 
         quantise_token_tile(0)
         quantise_token_tile(1)
-        nc.scalar.activation(out=warm[:], in_=eps[:], func=ACT.Sqrt)
+        nc.scalar.activation(out=warm[:], in_=eps[:], func=ACT.Abs_reciprocal_sqrt)
         for group in range(V_GROUP):
             project(0, group)
         quantise_token_tile(2)

@@ -21,18 +21,21 @@ DOUBLINGS = 6
 K_PASS = 512
 PASSES = C // K_PASS
 BANK = 512
+PSUM_BANKS = 8
 HEADS_PER_BANK = BANK // HEAD
 TILES_PER_BATCH = T // P
 TOKEN_TILES = BATCH * TILES_PER_BATCH
 CHUNK = 2 * BANK
-Q_GROUPS, K_GROUP, V_GROUP = 4, 4, 5
+GROUPS = 6
+K_GROUP, V_GROUP = 4, 5
+ROPE_BANKS = TOKEN_TILES * V_GROUP
 EPS = 1e-6
 ROPE_THETA = 10000.0
 SQUARE_SLICES = 8
 SMALL_COLUMNS = 2 * HEAD + 2
 ROUND_MAGIC = 1.5 * 2.0**23
 
-FLOPS = 2 * BATCH * T * C * (Q_GROUPS + 2) * BANK
+FLOPS = 2 * BATCH * T * C * GROUPS * BANK
 
 
 def tile_attention_pa_kernel(
@@ -47,12 +50,10 @@ def tile_attention_pa_kernel(
     v_rows = out_2.rearrange("b t h d -> (b t) (h d)")
 
     with tc.tile_pool(name="keep", bufs=1) as keep, \
-            tc.tile_pool(name="stage", bufs=2) as stage, \
-            tc.tile_pool(name="small", bufs=4) as small, \
-            tc.tile_pool(name="work", bufs=4) as work, \
+            tc.tile_pool(name="stage", bufs=TOKEN_TILES) as stage, \
+            tc.tile_pool(name="work", bufs=6) as work, \
             tc.tile_pool(name="results", bufs=8) as results, \
-            tc.psum_pool(name="psum_t", bufs=2) as psum_t, \
-            tc.psum_pool(name="psum_o", bufs=6) as psum_o, \
+            tc.psum_pool(name="psum", bufs=PSUM_BANKS) as psum, \
             tc.manual_schedule():
 
         x_sb = [keep.tile([P, C], BF16, name="x_sb%d" % m) for m in range(TOKEN_TILES)]
@@ -65,12 +66,12 @@ def tile_attention_pa_kernel(
             for m in range(TOKEN_TILES)
         ]
         w_words = [
-            keep.tile([P, PASSES, 2 * CHUNK], U8, name="w_words%d" % c, align_bytes=64)
-            for c in range(3)
+            keep.tile([P, PASSES, 2 * BANK], U8, name="w_words%d" % group, align_bytes=64)
+            for group in range(GROUPS)
         ]
         w_planes = [
             keep.tile([P, PASSES, CHUNK], U8, name="w_planes%d" % c, align_bytes=64)
-            for c in range(3)
+            for c in range(GROUPS // 2)
         ]
         v1_sb = keep.tile([P, TOKEN_TILES, BANK], BF16)
         small_row = keep.tile([P, SMALL_COLUMNS], BF16)
@@ -79,29 +80,31 @@ def tile_attention_pa_kernel(
         eps = keep.tile([P, 1], F32)
         warm = keep.tile([P, 1], F32)
         squares = keep.tile([P, SQUARE_SLICES, HEAD], F32)
-        squares_written = []
+        sum_squares = keep.tile([P, ROPE_BANKS, HEADS_PER_BANK], F32)
+        rstd = keep.tile([P, ROPE_BANKS, HEADS_PER_BANK], F32)
 
         def load_x(m):
             nc.sync.dma_start(out=x_sb[m][:], in_=x_rows[m * P:(m + 1) * P, :])
 
-        def load_weights(c, words, scales, first_column):
-            nc.vector.memset(w_planes[c][:].bitcast(I32), 0)
+        def load_scales(c, scales, first_column):
             scale_words = scales.bitcast(I32)[:, :, first_column // 4:(first_column + CHUNK) // 4]
-            for row in range(8):
-                partition = 32 * (row // 4) + row % 4
+            for row in range(4):
                 nc.sync.dma_start(
-                    out=w_planes[c][partition:P:64, :, :].bitcast(I32),
-                    in_=scale_words[:, row:16:8, :].rearrange("g q w -> q g w"),
+                    out=w_planes[c][row:P:32, :, :].bitcast(I32),
+                    in_=scale_words[:, row:16:4, :].rearrange("g q w -> q g w"),
                 )
+
+        def load_words(group, words, first_column):
             nc.sync.dma_start(
-                out=w_words[c][:].bitcast(I32),
-                in_=words.bitcast(I32)[:, :, first_column // 2:(first_column + CHUNK) // 2]
+                out=w_words[group][:].bitcast(I32),
+                in_=words.bitcast(I32)[:, :, first_column // 2:(first_column + BANK) // 2]
                 .rearrange("g p w -> p g w"),
             )
 
-        nc.vector.memset(eps[:], EPS)
         nc.vector.memset(small_row[:], 0.0)
+        nc.vector.memset(w_planes[0][:].bitcast(I32), 0)
         nc.vector.memset(ones[:], 1.0)
+        nc.vector.memset(eps[:], EPS)
         nc.scalar.dma_start(out=small_row[0:1, 0:HEAD], in_=q_scale.rearrange("(o n) -> o n", o=1))
         nc.scalar.dma_start(out=small_row[0:1, HEAD:2 * HEAD], in_=k_scale.rearrange("(o n) -> o n", o=1))
         nc.scalar.dma_start(
@@ -109,13 +112,17 @@ def tile_attention_pa_kernel(
         )
         nc.scalar.activation(out=warm[:], in_=eps[:], func=ACT.Sin)
 
-        make_identity(nc, identity[:])
         position_i = keep.tile([P, TILES_PER_BATCH], I32)
         nc.gpsimd.iota(position_i[:], pattern=[[P, TILES_PER_BATCH]], base=0, channel_multiplier=1)
+        make_identity(nc, identity[:])
 
         load_x(0)
+        load_scales(0, Wq_scales, 0)
+        load_words(0, Wq_words, 0)
         load_x(1)
-        load_weights(0, Wq_words, Wq_scales, 0)
+        load_words(1, Wq_words, BANK)
+        load_x(2)
+        load_x(3)
 
         freq = keep.tile([P, 4, HALF], F32)
         nc.vector.memset(freq[:, :, 0:1], 1.0)
@@ -149,20 +156,134 @@ def tile_attention_pa_kernel(
         nc.scalar.activation(
             out=trig[:].rearrange("p c j -> p (c j)"), in_=angle_flat, func=ACT.Sin
         )
+        nc.scalar.activation(out=warm[:], in_=eps[:], func=ACT.Abs_reciprocal_sqrt)
 
-        load_weights(1, Wq_words, Wq_scales, CHUNK)
-        load_weights(2, Wkv_words, Wkv_scales, 0)
-        load_x(2)
-        load_x(3)
+        nc.vector.memset(w_planes[1][:].bitcast(I32), 0)
+        nc.vector.memset(w_planes[2][:].bitcast(I32), 0)
+        load_scales(1, Wq_scales, CHUNK)
+        load_words(2, Wq_words, 2 * BANK)
+        load_words(3, Wq_words, 3 * BANK)
+        load_scales(2, Wkv_scales, 0)
+        load_words(K_GROUP, Wkv_words, 0)
+        load_words(V_GROUP, Wkv_words, BANK)
         nc.sync.dma_start(out=v1_sb[:], in_=v1_rows.rearrange("(m p) c -> p m c", p=P))
 
-        spread = psum_t.tile([P, BANK], F32, tag="turned")
+        def quantise_token_tile(m, copy_engines):
+            x_words = x_sb[m][:].bitcast(F32)
+            grouped = stage.tile([P, PASSES, P, 4], BF16, align_bytes=64)
+            grouped_words = grouped[:].bitcast(F32)
+            banks = []
+            for pair in range(PASSES // 2):
+                turned = psum.tile([P, 2, 2, P], F32, tag="bank")
+                for j in range(2):
+                    first_word = (K_PASS // 2) * (2 * pair + j)
+                    for u in range(2):
+                        nc.tensor.transpose(
+                            turned[:, j, u, :],
+                            x_words[:, first_word + u:first_word + K_PASS // 2:2],
+                            identity[:],
+                        )
+                banks.append(turned)
+            for pair in range(PASSES // 2):
+                destination = grouped_words[:, 2 * pair:2 * pair + 2, :, :]
+                source = banks[pair][:].rearrange("p j u r -> p j r u")
+                if copy_engines[pair] == "scalar":
+                    nc.scalar.copy(out=destination, in_=source)
+                else:
+                    nc.vector.tensor_copy(out=destination, in_=source)
+            for pair in range(PASSES // 2):
+                passes = slice(2 * pair, 2 * pair + 2)
+                nc.vector.quantize_mx(
+                    out=x_codes[m][:, passes, :].rearrange("p g r -> p (g r)").bitcast(FP8X4),
+                    scales=x_scales[m][:, passes, :].rearrange("p g r -> p (g r)"),
+                    in_=grouped[:, passes, :, :].rearrange("p g r t -> p (g r t)"),
+                )
+
+        def project(m, group):
+            acc = psum.tile([P, BANK], F32, tag="bank")
+            half = group % 2
+            for g in range(PASSES):
+                nc.tensor.matmul_mx(
+                    out=acc[:],
+                    lhsT=x_codes[m][:, g, :].bitcast(FP8X4),
+                    lhsT_scale=x_scales[m][:, g, :],
+                    rhs=w_words[group][:, g, :].bitcast(FP4X4),
+                    rhs_scale=w_planes[group // 2][:, g, BANK * half:BANK * (half + 1)],
+                    start=(g == 0),
+                    stop=(g == PASSES - 1),
+                )
+            return acc
+
+        def value_bank(m):
+            acc = project(m, V_GROUP)
+            result = results.tile([P, BANK], F32)
+            nc.vector.scalar_tensor_tensor(
+                out=result[:], in0=v1_sb[:, m, :], scalar=one_minus_lambda[:, 0:1],
+                in1=acc[:], op0=ALU.mult, op1=ALU.add,
+            )
+            nc.sync.dma_start(out=v_rows[m * P:(m + 1) * P, :], in_=result[:])
+
+        squares_written = []
+        waiting = []
+
+        def square(acc, n, h):
+            nc.scalar.activation(
+                out=squares[:, len(squares_written) % SQUARE_SLICES, :],
+                in_=acc[:, h * HEAD:(h + 1) * HEAD], func=ACT.Square,
+                accum_out=sum_squares[:, n, h:h + 1],
+            )
+            squares_written.append(h)
+
+        def finish_waiting_bank():
+            for acc, n, m, group in waiting:
+                nc.scalar.activation(
+                    out=rstd[:, n, :], in_=sum_squares[:, n, :], func=ACT.Abs_reciprocal_sqrt,
+                    bias=eps[:, 0:1], scale=1.0 / HEAD,
+                )
+                a = m % TILES_PER_BATCH
+                table = table_k if group == K_GROUP else table_q
+                products = work.tile([P, HEADS_PER_BANK, 2, HEAD], F32)
+                for h in range(HEADS_PER_BANK):
+                    nc.vector.scalar_tensor_tensor(
+                        out=products[:, h, :, :],
+                        in0=acc[:, h * HEAD:(h + 1) * HEAD].unsqueeze(1).to_broadcast([P, 2, HEAD]),
+                        scalar=rstd[:, n, h:h + 1],
+                        in1=table[:, 2 * a:2 * a + 2, :],
+                        op0=ALU.mult, op1=ALU.mult,
+                    )
+                terms = products[:].rearrange("p h o (s i) -> p (h o) s i", s=2)
+                result = results.tile([P, BANK], F32)
+                nc.gpsimd.tensor_tensor(
+                    out=result[:].rearrange("p (c i) -> p c i", i=HALF),
+                    in0=terms[:, :, 0, :], in1=terms[:, :, 1, :], op=ALU.add,
+                )
+                token_rows = slice(m * P, (m + 1) * P)
+                if group == K_GROUP:
+                    nc.sync.dma_start(out=k_rows[token_rows, :], in_=result[:])
+                else:
+                    nc.sync.dma_start(
+                        out=q_rows[token_rows, group * BANK:(group + 1) * BANK], in_=result[:]
+                    )
+            waiting.clear()
+
+        rope_banks_begun = []
+
+        def rope_bank(m, group):
+            n = len(rope_banks_begun)
+            rope_banks_begun.append(n)
+            acc = project(m, group)
+            square(acc, n, 0)
+            finish_waiting_bank()
+            for h in range(1, HEADS_PER_BANK):
+                square(acc, n, h)
+            waiting.append((acc, n, m, group))
+
+        quantise_token_tile(0, ("scalar", "vector"))
+
+        spread = psum.tile([P, BANK], F32, tag="bank")
         nc.tensor.matmul(
             out=spread[:, 0:SMALL_COLUMNS], lhsT=ones[:], rhs=small_row[:], start=True, stop=True
         )
-        gain_q = spread[:, 0:HEAD]
-        gain_k = spread[:, HEAD:2 * HEAD]
-        lam = spread[:, 2 * HEAD:2 * HEAD + 1]
 
         def rope_table(gain, name):
             table = keep.tile([P, TILES_PER_BATCH * 2, HEAD], F32, name=name)
@@ -173,109 +294,30 @@ def tile_attention_pa_kernel(
             )
             return table
 
-        table_q = rope_table(gain_q, "table_q")
-        table_k = rope_table(gain_k, "table_k")
+        table_q = rope_table(spread[:, 0:HEAD], "table_q")
+        table_k = rope_table(spread[:, HEAD:2 * HEAD], "table_k")
         one_minus_lambda = keep.tile([P, 1], F32)
         nc.vector.tensor_scalar(
-            out=one_minus_lambda[:], in0=lam, scalar1=-1.0, scalar2=1.0,
+            out=one_minus_lambda[:], in0=spread[:, 2 * HEAD:2 * HEAD + 1], scalar1=-1.0, scalar2=1.0,
             op0=ALU.mult, op1=ALU.add,
         )
 
-        def quantise_token_tile(m):
-            x_words = x_sb[m][:].bitcast(F32)
-            grouped = stage.tile([P, PASSES, P, 4], BF16, align_bytes=64)
-            grouped_words = grouped[:].bitcast(F32)
-            for pair in range(PASSES // 2):
-                turned = psum_t.tile([P, 2, 2, P], F32, tag="turned")
-                for j in range(2):
-                    first_word = (K_PASS // 2) * (2 * pair + j)
-                    for u in range(2):
-                        nc.tensor.transpose(
-                            turned[:, j, u, :],
-                            x_words[:, first_word + u:first_word + K_PASS // 2:2],
-                            identity[:],
-                        )
-                nc.scalar.copy(
-                    out=grouped_words[:, 2 * pair:2 * pair + 2, :, :],
-                    in_=turned[:].rearrange("p j u r -> p j r u"),
-                )
-            nc.vector.quantize_mx(
-                out=x_codes[m][:].rearrange("p g r -> p (g r)").bitcast(FP8X4),
-                scales=x_scales[m][:].rearrange("p g r -> p (g r)"),
-                in_=grouped[:].rearrange("p g r t -> p (g r t)"),
-            )
-
-        def mix_values(acc, m, result):
-            nc.vector.scalar_tensor_tensor(
-                out=result[:], in0=v1_sb[:, m, :], scalar=one_minus_lambda[:, 0:1],
-                in1=acc[:], op0=ALU.mult, op1=ALU.add,
-            )
-
-        def norm_and_rope(acc, a, table, result):
-            sum_squares = small.tile([P, HEADS_PER_BANK], F32)
-            for h in range(HEADS_PER_BANK):
-                nc.scalar.activation(
-                    out=squares[:, len(squares_written) % SQUARE_SLICES, :],
-                    in_=acc[:, h * HEAD:(h + 1) * HEAD], func=ACT.Square,
-                    accum_out=sum_squares[:, h:h + 1],
-                )
-                squares_written.append(h)
-            rstd = small.tile([P, HEADS_PER_BANK], F32)
-            nc.scalar.activation(
-                out=rstd[:], in_=sum_squares[:], func=ACT.Abs_reciprocal_sqrt,
-                bias=eps[:, 0:1], scale=1.0 / HEAD,
-            )
-            products = work.tile([P, HEADS_PER_BANK, 2, HEAD], F32)
-            for h in range(HEADS_PER_BANK):
-                nc.vector.scalar_tensor_tensor(
-                    out=products[:, h, :, :],
-                    in0=acc[:, h * HEAD:(h + 1) * HEAD].unsqueeze(1).to_broadcast([P, 2, HEAD]),
-                    scalar=rstd[:, h:h + 1],
-                    in1=table[:, 2 * a:2 * a + 2, :],
-                    op0=ALU.mult, op1=ALU.mult,
-                )
-            terms = products[:].rearrange("p h o (s i) -> p (h o) s i", s=2)
-            nc.gpsimd.tensor_tensor(
-                out=result[:].rearrange("p (c i) -> p c i", i=HALF),
-                in0=terms[:, :, 0, :], in1=terms[:, :, 1, :], op=ALU.add,
-            )
-
-        def project(batch, group):
-            chunk, half = group // 2, group % 2
-            for a in range(TILES_PER_BATCH):
-                m = batch * TILES_PER_BATCH + a
-                token_rows = slice(m * P, (m + 1) * P)
-                acc = psum_o.tile([P, BANK], F32)
-                for g in range(PASSES):
-                    nc.tensor.matmul_mx(
-                        out=acc[:],
-                        lhsT=x_codes[m][:, g, :].bitcast(FP8X4),
-                        lhsT_scale=x_scales[m][:, g, :],
-                        rhs=w_words[chunk][:, g, 2 * BANK * half:2 * BANK * (half + 1)].bitcast(FP4X4),
-                        rhs_scale=w_planes[chunk][:, g, BANK * half:BANK * (half + 1)],
-                        start=(g == 0),
-                        stop=(g == PASSES - 1),
-                    )
-                result = results.tile([P, BANK], F32)
-                if group == V_GROUP:
-                    mix_values(acc, m, result)
-                    nc.sync.dma_start(out=v_rows[token_rows, :], in_=result[:])
-                elif group == K_GROUP:
-                    norm_and_rope(acc, a, table_k, result)
-                    nc.sync.dma_start(out=k_rows[token_rows, :], in_=result[:])
-                else:
-                    norm_and_rope(acc, a, table_q, result)
-                    nc.sync.dma_start(
-                        out=q_rows[token_rows, group * BANK:(group + 1) * BANK], in_=result[:]
-                    )
-
-        quantise_token_tile(0)
-        quantise_token_tile(1)
-        nc.scalar.activation(out=warm[:], in_=eps[:], func=ACT.Abs_reciprocal_sqrt)
-        for group in range(V_GROUP):
-            project(0, group)
-        quantise_token_tile(2)
-        quantise_token_tile(3)
-        project(0, V_GROUP)
-        for group in range(V_GROUP + 1):
-            project(1, group)
+        rope_bank(0, 0)
+        finish_waiting_bank()
+        quantise_token_tile(1, ("scalar", "scalar"))
+        rope_bank(0, 1)
+        finish_waiting_bank()
+        quantise_token_tile(2, ("scalar", "scalar"))
+        rope_bank(1, 0)
+        rope_bank(1, 1)
+        finish_waiting_bank()
+        quantise_token_tile(3, ("scalar", "scalar"))
+        for m in (2, 3):
+            for group in (0, 1):
+                rope_bank(m, group)
+        for group in range(2, V_GROUP):
+            for m in range(TOKEN_TILES):
+                rope_bank(m, group)
+        finish_waiting_bank()
+        for m in range(TOKEN_TILES):
+            value_bank(m)

@@ -17,7 +17,7 @@ P = 128
 BATCH, T, C = 2, 256, 2048
 HEAD = 128
 HALF = HEAD // 2
-DOUBLINGS = 6
+FREQ_LEVELS = 3
 K_PASS = 512
 PASSES = C // K_PASS
 BANK = 512
@@ -101,10 +101,15 @@ def tile_attention_pa_kernel(
                 .rearrange("g p w -> p g w"),
             )
 
-        nc.vector.memset(small_row[:], 0.0)
-        nc.vector.memset(w_planes[0][:].bitcast(I32), 0)
-        nc.vector.memset(ones[:], 1.0)
         nc.vector.memset(eps[:], EPS)
+        nc.gpsimd.memset(small_row[:], 0.0)
+        position_i = keep.tile([P, TILES_PER_BATCH], I32)
+        nc.gpsimd.iota(position_i[:], pattern=[[P, TILES_PER_BATCH]], base=0, channel_multiplier=1)
+        nc.gpsimd.memset(w_planes[0][:].bitcast(F32), 0.0)
+        make_identity(nc, identity[:])
+        nc.gpsimd.memset(ones[:], 1.0)
+        nc.gpsimd.memset(w_planes[1][:].bitcast(F32), 0.0)
+        nc.gpsimd.memset(w_planes[2][:].bitcast(F32), 0.0)
         nc.scalar.dma_start(out=small_row[0:1, 0:HEAD], in_=q_scale.rearrange("(o n) -> o n", o=1))
         nc.scalar.dma_start(out=small_row[0:1, HEAD:2 * HEAD], in_=k_scale.rearrange("(o n) -> o n", o=1))
         nc.scalar.dma_start(
@@ -112,9 +117,6 @@ def tile_attention_pa_kernel(
         )
         nc.scalar.activation(out=warm[:], in_=eps[:], func=ACT.Sin)
 
-        position_i = keep.tile([P, TILES_PER_BATCH], I32)
-        nc.gpsimd.iota(position_i[:], pattern=[[P, TILES_PER_BATCH]], base=0, channel_multiplier=1)
-        make_identity(nc, identity[:])
 
         load_x(0)
         load_scales(0, Wq_scales, 0)
@@ -127,39 +129,38 @@ def tile_attention_pa_kernel(
         freq = keep.tile([P, 4, HALF], F32)
         nc.vector.memset(freq[:, :, 0:1], 1.0)
         nc.vector.memset(freq[:, 1:2, 0:1], -1.0)
-        for doubling in range(DOUBLINGS):
-            step = 2 ** doubling
-            nc.vector.tensor_scalar_mul(
-                out=freq[:, :, step:2 * step], in0=freq[:, :, 0:step],
-                scalar1=ROPE_THETA ** (-step / HALF),
-            )
-        position = keep.tile([P, TILES_PER_BATCH], F32)
-        nc.vector.tensor_copy(out=position[:], in_=position_i[:])
-        angle = keep.tile([P, TILES_PER_BATCH, 4, HALF], F32)
+        for level in range(FREQ_LEVELS):
+            width = 4 ** level
+            for j in range(1, 4):
+                nc.vector.tensor_scalar_mul(
+                    out=freq[:, :, j * width:(j + 1) * width], in0=freq[:, :, 0:width],
+                    scalar1=ROPE_THETA ** (-(j * width) / HALF),
+                )
+        position_turns = keep.tile([P, TILES_PER_BATCH], F32)
+        nc.vector.tensor_scalar_mul(out=position_turns[:], in0=position_i[:], scalar1=1.0 / (2.0 * math.pi))
+        turn = keep.tile([P, TILES_PER_BATCH, 4, HALF], F32)
         for a in range(TILES_PER_BATCH):
-            nc.vector.tensor_scalar_mul(out=angle[:, a, :, :], in0=freq[:], scalar1=position[:, a:a + 1])
-        nc.vector.tensor_scalar_add(
-            out=angle[:, :, 0:4:3, :], in0=angle[:, :, 0:4:3, :], scalar1=math.pi / 2
+            nc.vector.tensor_scalar(
+                out=turn[:, a, 0:4:3, :], in0=freq[:, 0:4:3, :], scalar1=position_turns[:, a:a + 1],
+                scalar2=0.25, op0=ALU.mult, op1=ALU.add,
+            )
+            nc.vector.tensor_scalar_mul(
+                out=turn[:, a, 1:3, :], in0=freq[:, 1:3, :], scalar1=position_turns[:, a:a + 1]
+            )
+        turn_flat = turn[:].rearrange("p a b i -> p (a b i)")
+        shifted = keep.tile([P, TILES_PER_BATCH * 4 * HALF], F32)
+        nc.vector.tensor_scalar_add(out=shifted[:], in0=turn_flat, scalar1=ROUND_MAGIC)
+        whole_less_turn = keep.tile([P, TILES_PER_BATCH * 4 * HALF], F32)
+        nc.vector.scalar_tensor_tensor(
+            out=whole_less_turn[:], in0=shifted[:], scalar=ROUND_MAGIC, in1=turn_flat,
+            op0=ALU.subtract, op1=ALU.subtract,
         )
-        angle_flat = angle[:].rearrange("p a b i -> p (a b i)")
-        turns = keep.tile([P, TILES_PER_BATCH * 4 * HALF], F32)
-        nc.vector.tensor_scalar(
-            out=turns[:], in0=angle_flat, scalar1=1.0 / (2.0 * math.pi), scalar2=ROUND_MAGIC,
-            op0=ALU.mult, op1=ALU.add,
-        )
-        nc.vector.tensor_scalar(
-            out=turns[:], in0=turns[:], scalar1=ROUND_MAGIC, scalar2=-2.0 * math.pi,
-            op0=ALU.subtract, op1=ALU.mult,
-        )
-        nc.vector.tensor_tensor(out=angle_flat, in0=angle_flat, in1=turns[:], op=ALU.add)
         trig = keep.tile([P, TILES_PER_BATCH * 2, HEAD], F32)
         nc.scalar.activation(
-            out=trig[:].rearrange("p c j -> p (c j)"), in_=angle_flat, func=ACT.Sin
+            out=trig[:].rearrange("p c j -> p (c j)"), in_=whole_less_turn[:], func=ACT.Sin,
+            scale=-2.0 * math.pi,
         )
-        nc.scalar.activation(out=warm[:], in_=eps[:], func=ACT.Abs_reciprocal_sqrt)
 
-        nc.vector.memset(w_planes[1][:].bitcast(I32), 0)
-        nc.vector.memset(w_planes[2][:].bitcast(I32), 0)
         load_scales(1, Wq_scales, CHUNK)
         load_words(2, Wq_words, 2 * BANK)
         load_words(3, Wq_words, 3 * BANK)
@@ -279,6 +280,7 @@ def tile_attention_pa_kernel(
             waiting.append((acc, n, m, group))
 
         quantise_token_tile(0, ("scalar", "vector"))
+        nc.scalar.activation(out=warm[:], in_=eps[:], func=ACT.Abs_reciprocal_sqrt)
 
         spread = psum.tile([P, BANK], F32, tag="bank")
         nc.tensor.matmul(

@@ -247,9 +247,9 @@ def tile_attention_pa_kernel(
                 for h in range(HEADS_PER_BANK):
                     nc.vector.scalar_tensor_tensor(
                         out=products[:, h, :, :],
-                        in0=acc[:, h * HEAD:(h + 1) * HEAD].unsqueeze(1).to_broadcast([P, 2, HEAD]),
+                        in0=table[:, 2 * a:2 * a + 2, :],
                         scalar=rstd[:, n, h:h + 1],
-                        in1=table[:, 2 * a:2 * a + 2, :],
+                        in1=acc[:, h * HEAD:(h + 1) * HEAD].unsqueeze(1).to_broadcast([P, 2, HEAD]),
                         op0=ALU.mult, op1=ALU.mult,
                     )
                 terms = products[:].rearrange("p h o (s i) -> p (h o) s i", s=2)

@@ -102,14 +102,12 @@ def tile_attention_pa_kernel(
             )
 
         nc.vector.memset(eps[:], EPS)
-        nc.gpsimd.memset(small_row[:], 0.0)
+        nc.vector.memset(small_row[:], 0.0)
+        nc.vector.memset(w_planes[0][:].bitcast(I32), 0)
+        nc.vector.memset(ones[:], 1.0)
         position_i = keep.tile([P, TILES_PER_BATCH], I32)
         nc.gpsimd.iota(position_i[:], pattern=[[P, TILES_PER_BATCH]], base=0, channel_multiplier=1)
-        nc.gpsimd.memset(w_planes[0][:].bitcast(F32), 0.0)
         make_identity(nc, identity[:])
-        nc.gpsimd.memset(ones[:], 1.0)
-        nc.gpsimd.memset(w_planes[1][:].bitcast(F32), 0.0)
-        nc.gpsimd.memset(w_planes[2][:].bitcast(F32), 0.0)
         nc.scalar.dma_start(out=small_row[0:1, 0:HEAD], in_=q_scale.rearrange("(o n) -> o n", o=1))
         nc.scalar.dma_start(out=small_row[0:1, HEAD:2 * HEAD], in_=k_scale.rearrange("(o n) -> o n", o=1))
         nc.scalar.dma_start(
@@ -118,13 +116,11 @@ def tile_attention_pa_kernel(
         nc.scalar.activation(out=warm[:], in_=eps[:], func=ACT.Sin)
 
 
-        load_x(0)
+        for m in range(TOKEN_TILES):
+            load_x(m)
         load_scales(0, Wq_scales, 0)
         load_words(0, Wq_words, 0)
-        load_x(1)
         load_words(1, Wq_words, BANK)
-        load_x(2)
-        load_x(3)
 
         freq = keep.tile([P, 4, HALF], F32)
         nc.vector.memset(freq[:, :, 0:1], 1.0)
@@ -161,6 +157,8 @@ def tile_attention_pa_kernel(
             scale=-2.0 * math.pi,
         )
 
+        nc.vector.memset(w_planes[1][:].bitcast(I32), 0)
+        nc.vector.memset(w_planes[2][:].bitcast(I32), 0)
         load_scales(1, Wq_scales, CHUNK)
         load_words(2, Wq_words, 2 * BANK)
         load_words(3, Wq_words, 3 * BANK)
@@ -279,7 +277,8 @@ def tile_attention_pa_kernel(
                 square(acc, n, h)
             waiting.append((acc, n, m, group))
 
-        quantise_token_tile(0, ("scalar", "vector"))
+        for m in range(TOKEN_TILES):
+            quantise_token_tile(m, ("scalar", "vector"))
         nc.scalar.activation(out=warm[:], in_=eps[:], func=ACT.Abs_reciprocal_sqrt)
 
         spread = psum.tile([P, BANK], F32, tag="bank")
@@ -304,20 +303,7 @@ def tile_attention_pa_kernel(
             op0=ALU.mult, op1=ALU.add,
         )
 
-        rope_bank(0, 0)
-        finish_waiting_bank()
-        quantise_token_tile(1, ("scalar", "scalar"))
-        rope_bank(0, 1)
-        finish_waiting_bank()
-        quantise_token_tile(2, ("scalar", "scalar"))
-        rope_bank(1, 0)
-        rope_bank(1, 1)
-        finish_waiting_bank()
-        quantise_token_tile(3, ("scalar", "scalar"))
-        for m in (2, 3):
-            for group in (0, 1):
-                rope_bank(m, group)
-        for group in range(2, V_GROUP):
+        for group in range(V_GROUP):
             for m in range(TOKEN_TILES):
                 rope_bank(m, group)
         finish_waiting_bank()

@@ -32,6 +32,8 @@ ROPE_BANKS = TOKEN_TILES * V_GROUP
 EPS = 1e-6
 ROPE_THETA = 10000.0
 SQUARE_SLICES = 8
+WARM_BEFORE_X = 6
+WARM_BETWEEN = 2
 SMALL_COLUMNS = 2 * HEAD + 2
 ROUND_MAGIC = 1.5 * 2.0**23
 
@@ -75,7 +77,7 @@ def tile_attention_pa_kernel(
         ]
         v1_sb = keep.tile([P, TOKEN_TILES, BANK], BF16)
         small_row = keep.tile([P, SMALL_COLUMNS], BF16)
-        ones = keep.tile([P, P], BF16)
+        ones = keep.tile([P, BANK], BF16)
         identity = keep.tile([P, P], F32)
         eps = keep.tile([P, 1], F32)
         warm = keep.tile([P, 1], F32)
@@ -102,9 +104,9 @@ def tile_attention_pa_kernel(
             )
 
         nc.vector.memset(eps[:], EPS)
+        nc.vector.memset(ones[:], 1.0)
         nc.vector.memset(small_row[:], 0.0)
         nc.vector.memset(w_planes[0][:].bitcast(I32), 0)
-        nc.vector.memset(ones[:], 1.0)
         position_i = keep.tile([P, TILES_PER_BATCH], I32)
         nc.gpsimd.iota(position_i[:], pattern=[[P, TILES_PER_BATCH]], base=0, channel_multiplier=1)
         make_identity(nc, identity[:])
@@ -166,6 +168,14 @@ def tile_attention_pa_kernel(
         load_words(K_GROUP, Wkv_words, 0)
         load_words(V_GROUP, Wkv_words, BANK)
         nc.sync.dma_start(out=v1_sb[:], in_=v1_rows.rearrange("(m p) c -> p m c", p=P))
+
+        def keep_clock_up(count):
+            unread = psum.tile([P, BANK], F32, tag="bank")
+            for repeat in range(count):
+                nc.tensor.matmul(
+                    out=unread[:], lhsT=ones[:, 0:P], rhs=ones[:],
+                    start=(repeat == 0), stop=(repeat == count - 1),
+                )
 
         def quantise_token_tile(m, copy_engines):
             x_words = x_sb[m][:].bitcast(F32)
@@ -277,13 +287,16 @@ def tile_attention_pa_kernel(
                 square(acc, n, h)
             waiting.append((acc, n, m, group))
 
+        keep_clock_up(WARM_BEFORE_X)
         for m in range(TOKEN_TILES):
             quantise_token_tile(m, ("scalar", "vector"))
+            if m % 2 == 1:
+                keep_clock_up(WARM_BETWEEN)
         nc.scalar.activation(out=warm[:], in_=eps[:], func=ACT.Abs_reciprocal_sqrt)
 
         spread = psum.tile([P, BANK], F32, tag="bank")
         nc.tensor.matmul(
-            out=spread[:, 0:SMALL_COLUMNS], lhsT=ones[:], rhs=small_row[:], start=True, stop=True
+            out=spread[:, 0:SMALL_COLUMNS], lhsT=ones[:, 0:P], rhs=small_row[:], start=True, stop=True
         )
 
         def rope_table(gain, name):

@@ -32,6 +32,9 @@ ROPE_BANKS = TOKEN_TILES * V_GROUP
 EPS = 1e-6
 ROPE_THETA = 10000.0
 SQUARE_SLICES = 8
+SINGLE_FIRST = 6
+SINGLE_LAST = 2
+ROOT_AT_ONCE = 2
 WARM_BEFORE_X = 6
 WARM_BETWEEN = 2
 SMALL_COLUMNS = 2 * HEAD + 2
@@ -53,8 +56,8 @@ def tile_attention_pa_kernel(
 
     with tc.tile_pool(name="keep", bufs=1) as keep, \
             tc.tile_pool(name="stage", bufs=TOKEN_TILES) as stage, \
-            tc.tile_pool(name="work", bufs=6) as work, \
-            tc.tile_pool(name="results", bufs=8) as results, \
+            tc.tile_pool(name="work", bufs=3) as work, \
+            tc.tile_pool(name="results", bufs=4) as results, \
             tc.psum_pool(name="psum", bufs=PSUM_BANKS) as psum, \
             tc.manual_schedule():
 
@@ -103,64 +106,77 @@ def tile_attention_pa_kernel(
                 .rearrange("g p w -> p g w"),
             )
 
+        def load_words_by_pass(group, words, first_column):
+            for g in range(PASSES):
+                nc.sync.dma_start(
+                    out=w_words[group][:, g, :].bitcast(I32),
+                    in_=words.bitcast(I32)[g, :, first_column // 2:(first_column + BANK) // 2],
+                )
+
         nc.vector.memset(eps[:], EPS)
         nc.vector.memset(ones[:], 1.0)
-        nc.vector.memset(small_row[:], 0.0)
-        nc.vector.memset(w_planes[0][:].bitcast(I32), 0)
         position_i = keep.tile([P, TILES_PER_BATCH], I32)
         nc.gpsimd.iota(position_i[:], pattern=[[P, TILES_PER_BATCH]], base=0, channel_multiplier=1)
         make_identity(nc, identity[:])
-        nc.scalar.dma_start(out=small_row[0:1, 0:HEAD], in_=q_scale.rearrange("(o n) -> o n", o=1))
-        nc.scalar.dma_start(out=small_row[0:1, HEAD:2 * HEAD], in_=k_scale.rearrange("(o n) -> o n", o=1))
-        nc.scalar.dma_start(
-            out=small_row[0:1, 2 * HEAD:2 * HEAD + 1], in_=value_lambda.rearrange("(o n) -> o n", o=1)
-        )
         nc.scalar.activation(out=warm[:], in_=eps[:], func=ACT.Sin)
-
-
         for m in range(TOKEN_TILES):
             load_x(m)
-        load_scales(0, Wq_scales, 0)
-        load_words(0, Wq_words, 0)
-        load_words(1, Wq_words, BANK)
 
         freq = keep.tile([P, 4, HALF], F32)
         nc.vector.memset(freq[:, :, 0:1], 1.0)
         nc.vector.memset(freq[:, 1:2, 0:1], -1.0)
-        for level in range(FREQ_LEVELS):
+
+        def freq_level(level):
             width = 4 ** level
             for j in range(1, 4):
                 nc.vector.tensor_scalar_mul(
                     out=freq[:, :, j * width:(j + 1) * width], in0=freq[:, :, 0:width],
                     scalar1=ROPE_THETA ** (-(j * width) / HALF),
                 )
+
+        freq_level(0)
+        nc.vector.memset(small_row[:], 0.0)
+        nc.scalar.dma_start(out=small_row[0:1, 0:HEAD], in_=q_scale.rearrange("(o n) -> o n", o=1))
+        nc.scalar.dma_start(out=small_row[0:1, HEAD:2 * HEAD], in_=k_scale.rearrange("(o n) -> o n", o=1))
+        nc.scalar.dma_start(
+            out=small_row[0:1, 2 * HEAD:2 * HEAD + 1], in_=value_lambda.rearrange("(o n) -> o n", o=1)
+        )
+        freq_level(1)
+        nc.vector.memset(w_planes[0][:].bitcast(I32), 0)
+        load_scales(0, Wq_scales, 0)
+        load_words_by_pass(0, Wq_words, 0)
+        load_words(1, Wq_words, BANK)
+        freq_level(2)
         position_turns = keep.tile([P, TILES_PER_BATCH], F32)
         nc.vector.tensor_scalar_mul(out=position_turns[:], in0=position_i[:], scalar1=1.0 / (2.0 * math.pi))
-        turn = keep.tile([P, TILES_PER_BATCH, 4, HALF], F32)
+        nc.vector.memset(w_planes[1][:].bitcast(I32), 0)
+        turn = keep.tile([P, TILES_PER_BATCH, 4 * HALF], F32)
         for a in range(TILES_PER_BATCH):
+            blocks = turn[:, a, :].rearrange("p (b i) -> p b i", i=HALF)
             nc.vector.tensor_scalar(
-                out=turn[:, a, 0:4:3, :], in0=freq[:, 0:4:3, :], scalar1=position_turns[:, a:a + 1],
+                out=blocks[:, 0:4:3, :], in0=freq[:, 0:4:3, :], scalar1=position_turns[:, a:a + 1],
                 scalar2=0.25, op0=ALU.mult, op1=ALU.add,
             )
             nc.vector.tensor_scalar_mul(
-                out=turn[:, a, 1:3, :], in0=freq[:, 1:3, :], scalar1=position_turns[:, a:a + 1]
+                out=blocks[:, 1:3, :], in0=freq[:, 1:3, :], scalar1=position_turns[:, a:a + 1]
             )
-        turn_flat = turn[:].rearrange("p a b i -> p (a b i)")
-        shifted = keep.tile([P, TILES_PER_BATCH * 4 * HALF], F32)
-        nc.vector.tensor_scalar_add(out=shifted[:], in0=turn_flat, scalar1=ROUND_MAGIC)
-        whole_less_turn = keep.tile([P, TILES_PER_BATCH * 4 * HALF], F32)
-        nc.vector.scalar_tensor_tensor(
-            out=whole_less_turn[:], in0=shifted[:], scalar=ROUND_MAGIC, in1=turn_flat,
-            op0=ALU.subtract, op1=ALU.subtract,
-        )
+        nc.vector.memset(w_planes[2][:].bitcast(I32), 0)
+        shifted = keep.tile([P, TILES_PER_BATCH, 4 * HALF], F32)
+        whole_less_turn = keep.tile([P, TILES_PER_BATCH, 4 * HALF], F32)
+        for a in range(TILES_PER_BATCH):
+            nc.vector.tensor_scalar_add(out=shifted[:, a, :], in0=turn[:, a, :], scalar1=ROUND_MAGIC)
+        for a in range(TILES_PER_BATCH):
+            nc.vector.scalar_tensor_tensor(
+                out=whole_less_turn[:, a, :], in0=shifted[:, a, :], scalar=ROUND_MAGIC,
+                in1=turn[:, a, :], op0=ALU.subtract, op1=ALU.subtract,
+            )
         trig = keep.tile([P, TILES_PER_BATCH * 2, HEAD], F32)
         nc.scalar.activation(
-            out=trig[:].rearrange("p c j -> p (c j)"), in_=whole_less_turn[:], func=ACT.Sin,
+            out=trig[:].rearrange("p c j -> p (c j)"),
+            in_=whole_less_turn[:].rearrange("p a c -> p (a c)"), func=ACT.Sin,
             scale=-2.0 * math.pi,
         )
 
-        nc.vector.memset(w_planes[1][:].bitcast(I32), 0)
-        nc.vector.memset(w_planes[2][:].bitcast(I32), 0)
         load_scales(1, Wq_scales, CHUNK)
         load_words(2, Wq_words, 2 * BANK)
         load_words(3, Wq_words, 3 * BANK)
@@ -177,9 +193,12 @@ def tile_attention_pa_kernel(
                     start=(repeat == 0), stop=(repeat == count - 1),
                 )
 
-        def quantise_token_tile(m, copy_engines):
+        grouped_tiles = {}
+
+        def transpose_token_tile(m, copy_engines):
             x_words = x_sb[m][:].bitcast(F32)
             grouped = stage.tile([P, PASSES, P, 4], BF16, align_bytes=64)
+            grouped_tiles[m] = grouped
             grouped_words = grouped[:].bitcast(F32)
             banks = []
             for pair in range(PASSES // 2):
@@ -200,13 +219,13 @@ def tile_attention_pa_kernel(
                     nc.scalar.copy(out=destination, in_=source)
                 else:
                     nc.vector.tensor_copy(out=destination, in_=source)
-            for pair in range(PASSES // 2):
-                passes = slice(2 * pair, 2 * pair + 2)
-                nc.vector.quantize_mx(
-                    out=x_codes[m][:, passes, :].rearrange("p g r -> p (g r)").bitcast(FP8X4),
-                    scales=x_scales[m][:, passes, :].rearrange("p g r -> p (g r)"),
-                    in_=grouped[:, passes, :, :].rearrange("p g r t -> p (g r t)"),
-                )
+
+        def quantise_token_tile(m):
+            nc.vector.quantize_mx(
+                out=x_codes[m][:].rearrange("p g r -> p (g r)").bitcast(FP8X4),
+                scales=x_scales[m][:].rearrange("p g r -> p (g r)"),
+                in_=grouped_tiles[m][:].rearrange("p g r t -> p (g r t)"),
+            )
 
         def project(m, group):
             acc = psum.tile([P, BANK], F32, tag="bank")
@@ -225,7 +244,7 @@ def tile_attention_pa_kernel(
 
         def value_bank(m):
             acc = project(m, V_GROUP)
-            result = results.tile([P, BANK], F32)
+            result = results.tile([P, BANK], F32, tag="value_result", bufs=TOKEN_TILES)
             nc.vector.scalar_tensor_tensor(
                 out=result[:], in0=v1_sb[:, m, :], scalar=one_minus_lambda[:, 0:1],
                 in1=acc[:], op0=ALU.mult, op1=ALU.add,
@@ -243,6 +262,22 @@ def tile_attention_pa_kernel(
             )
             squares_written.append(h)
 
+        left_for_vector = []
+        open_batch = []
+
+        def add_and_store(engine, products, result, first_tile, tiles, group):
+            terms = products.rearrange("p j h o (s i) -> p (j h o) s i", s=2)
+            engine.tensor_tensor(
+                out=result.rearrange("p j (c i) -> p (j c) i", i=HALF),
+                in0=terms[:, :, 0, :], in1=terms[:, :, 1, :], op=ALU.add,
+            )
+            token_rows = slice(first_tile * P, (first_tile + tiles) * P)
+            if group == K_GROUP:
+                rows = k_rows[token_rows, :]
+            else:
+                rows = q_rows[token_rows, group * BANK:(group + 1) * BANK]
+            nc.sync.dma_start(out=rows.rearrange("(j p) c -> p j c", p=P), in_=result)
+
         def finish_waiting_bank():
             for acc, n, m, group in waiting:
                 nc.scalar.activation(
@@ -251,28 +286,34 @@ def tile_attention_pa_kernel(
                 )
                 a = m % TILES_PER_BATCH
                 table = table_k if group == K_GROUP else table_q
-                products = work.tile([P, HEADS_PER_BANK, 2, HEAD], F32)
+                paired = SINGLE_FIRST <= n < ROPE_BANKS - SINGLE_LAST
+                j = m % 2 if paired else 0
+                if not paired:
+                    products = work.tile([P, 1, HEADS_PER_BANK, 2, HEAD], F32, tag="products1", bufs=3)
+                    result = results.tile([P, 1, BANK], F32, tag="result1", bufs=4)
+                    open_batch.append((products, result))
+                elif j == 0:
+                    products = work.tile([P, 2, HEADS_PER_BANK, 2, HEAD], F32, tag="products2", bufs=3)
+                    result = results.tile([P, 2, BANK], F32, tag="result2", bufs=4)
+                    open_batch.append((products, result))
+                products, result = open_batch[0]
                 for h in range(HEADS_PER_BANK):
                     nc.vector.scalar_tensor_tensor(
-                        out=products[:, h, :, :],
+                        out=products[:, j, h, :, :],
                         in0=table[:, 2 * a:2 * a + 2, :],
                         scalar=rstd[:, n, h:h + 1],
                         in1=acc[:, h * HEAD:(h + 1) * HEAD].unsqueeze(1).to_broadcast([P, 2, HEAD]),
                         op0=ALU.mult, op1=ALU.mult,
                     )
-                terms = products[:].rearrange("p h o (s i) -> p (h o) s i", s=2)
-                result = results.tile([P, BANK], F32)
-                nc.gpsimd.tensor_tensor(
-                    out=result[:].rearrange("p (c i) -> p c i", i=HALF),
-                    in0=terms[:, :, 0, :], in1=terms[:, :, 1, :], op=ALU.add,
-                )
-                token_rows = slice(m * P, (m + 1) * P)
-                if group == K_GROUP:
-                    nc.sync.dma_start(out=k_rows[token_rows, :], in_=result[:])
-                else:
-                    nc.sync.dma_start(
-                        out=q_rows[token_rows, group * BANK:(group + 1) * BANK], in_=result[:]
-                    )
+                if n == ROPE_BANKS - 1:
+                    left_for_vector.append((products, result, m, group))
+                    open_batch.clear()
+                elif not paired:
+                    add_and_store(nc.gpsimd, products[:], result[:], m, 1, group)
+                    open_batch.clear()
+                elif j == 1:
+                    add_and_store(nc.gpsimd, products[:], result[:], m - 1, 2, group)
+                    open_batch.clear()
             waiting.clear()
 
         rope_banks_begun = []
@@ -286,13 +327,15 @@ def tile_attention_pa_kernel(
             for h in range(1, HEADS_PER_BANK):
                 square(acc, n, h)
             waiting.append((acc, n, m, group))
+            if n < ROOT_AT_ONCE:
+                finish_waiting_bank()
 
         keep_clock_up(WARM_BEFORE_X)
-        for m in range(TOKEN_TILES):
-            quantise_token_tile(m, ("scalar", "vector"))
-            if m % 2 == 1:
-                keep_clock_up(WARM_BETWEEN)
+        transpose_token_tile(0, ("scalar", "vector"))
+        quantise_token_tile(0)
         nc.scalar.activation(out=warm[:], in_=eps[:], func=ACT.Abs_reciprocal_sqrt)
+        transpose_token_tile(1, ("scalar", "vector"))
+        keep_clock_up(WARM_BETWEEN)
 
         spread = psum.tile([P, BANK], F32, tag="bank")
         nc.tensor.matmul(
@@ -315,6 +358,12 @@ def tile_attention_pa_kernel(
             out=one_minus_lambda[:], in0=spread[:, 2 * HEAD:2 * HEAD + 1], scalar1=-1.0, scalar2=1.0,
             op0=ALU.mult, op1=ALU.add,
         )
+        quantise_token_tile(1)
+        transpose_token_tile(2, ("scalar", "vector"))
+        quantise_token_tile(2)
+        transpose_token_tile(3, ("scalar", "scalar"))
+        keep_clock_up(WARM_BETWEEN)
+        quantise_token_tile(3)
 
         for group in range(V_GROUP):
             for m in range(TOKEN_TILES):
@@ -322,3 +371,5 @@ def tile_attention_pa_kernel(
         finish_waiting_bank()
         for m in range(TOKEN_TILES):
             value_bank(m)
+        for products, result, m, group in left_for_vector:
+            add_and_store(nc.vector, products[:], result[:], m, 1, group)

@@ -249,7 +249,7 @@ def tile_attention_pa_kernel(
                 out=result[:], in0=v1_sb[:, m, :], scalar=one_minus_lambda[:, 0:1],
                 in1=acc[:], op0=ALU.mult, op1=ALU.add,
             )
-            nc.sync.dma_start(out=v_rows[m * P:(m + 1) * P, :], in_=result[:])
+            nc.scalar.dma_start(out=v_rows[m * P:(m + 1) * P, :], in_=result[:])
 
         squares_written = []
         waiting = []

@@ -35,7 +35,7 @@ SQUARE_SLICES = 8
 SINGLE_FIRST = 6
 SINGLE_LAST = 2
 ROOT_AT_ONCE = 2
-WARM_BEFORE_X = 6
+WARM_BEFORE_X = 4
 WARM_BETWEEN = 2
 SMALL_COLUMNS = 2 * HEAD + 2
 ROUND_MAGIC = 1.5 * 2.0**23
@@ -88,8 +88,11 @@ def tile_attention_pa_kernel(
         sum_squares = keep.tile([P, ROPE_BANKS, HEADS_PER_BANK], F32)
         rstd = keep.tile([P, ROPE_BANKS, HEADS_PER_BANK], F32)
 
-        def load_x(m):
-            nc.sync.dma_start(out=x_sb[m][:], in_=x_rows[m * P:(m + 1) * P, :])
+        def load_x(m, pieces=1):
+            width = C // pieces
+            for piece in range(pieces):
+                columns = slice(piece * width, (piece + 1) * width)
+                nc.sync.dma_start(out=x_sb[m][:, columns], in_=x_rows[m * P:(m + 1) * P, columns])
 
         def load_scales(c, scales, first_column):
             scale_words = scales.bitcast(I32)[:, :, first_column // 4:(first_column + CHUNK) // 4]
@@ -119,8 +122,10 @@ def tile_attention_pa_kernel(
         nc.gpsimd.iota(position_i[:], pattern=[[P, TILES_PER_BATCH]], base=0, channel_multiplier=1)
         make_identity(nc, identity[:])
         nc.scalar.activation(out=warm[:], in_=eps[:], func=ACT.Sin)
-        for m in range(TOKEN_TILES):
-            load_x(m)
+        load_x(0, 2)
+        load_x(1)
+        load_x(2)
+        load_x(3, 2)
 
         freq = keep.tile([P, 4, HALF], F32)
         nc.vector.memset(freq[:, :, 0:1], 1.0)
@@ -146,10 +151,21 @@ def tile_attention_pa_kernel(
         load_scales(0, Wq_scales, 0)
         load_words_by_pass(0, Wq_words, 0)
         load_words(1, Wq_words, BANK)
+        for c in (1, 2):
+            nc.sync.dma_start(
+                out=w_planes[c][:].rearrange("p g n -> p (g n)").bitcast(I32),
+                in_=Wq_words.bitcast(I32)[0, :, :],
+            )
+        load_words(2, Wq_words, 2 * BANK)
+        load_words(3, Wq_words, 3 * BANK)
+        load_scales(1, Wq_scales, CHUNK)
+        load_words(K_GROUP, Wkv_words, 0)
+        load_words(V_GROUP, Wkv_words, BANK)
+        load_scales(2, Wkv_scales, 0)
+        nc.sync.dma_start(out=v1_sb[:], in_=v1_rows.rearrange("(m p) c -> p m c", p=P))
         freq_level(2)
         position_turns = keep.tile([P, TILES_PER_BATCH], F32)
         nc.vector.tensor_scalar_mul(out=position_turns[:], in0=position_i[:], scalar1=1.0 / (2.0 * math.pi))
-        nc.vector.memset(w_planes[1][:].bitcast(I32), 0)
         turn = keep.tile([P, TILES_PER_BATCH, 4 * HALF], F32)
         for a in range(TILES_PER_BATCH):
             blocks = turn[:, a, :].rearrange("p (b i) -> p b i", i=HALF)
@@ -160,7 +176,6 @@ def tile_attention_pa_kernel(
             nc.vector.tensor_scalar_mul(
                 out=blocks[:, 1:3, :], in0=freq[:, 1:3, :], scalar1=position_turns[:, a:a + 1]
             )
-        nc.vector.memset(w_planes[2][:].bitcast(I32), 0)
         shifted = keep.tile([P, TILES_PER_BATCH, 4 * HALF], F32)
         whole_less_turn = keep.tile([P, TILES_PER_BATCH, 4 * HALF], F32)
         for a in range(TILES_PER_BATCH):
@@ -176,14 +191,6 @@ def tile_attention_pa_kernel(
             in_=whole_less_turn[:].rearrange("p a c -> p (a c)"), func=ACT.Sin,
             scale=-2.0 * math.pi,
         )
-
-        load_scales(1, Wq_scales, CHUNK)
-        load_words(2, Wq_words, 2 * BANK)
-        load_words(3, Wq_words, 3 * BANK)
-        load_scales(2, Wkv_scales, 0)
-        load_words(K_GROUP, Wkv_words, 0)
-        load_words(V_GROUP, Wkv_words, BANK)
-        nc.sync.dma_start(out=v1_sb[:], in_=v1_rows.rearrange("(m p) c -> p m c", p=P))
 
         def keep_clock_up(count):
             unread = psum.tile([P, BANK], F32, tag="bank")
@@ -278,23 +285,27 @@ def tile_attention_pa_kernel(
                 rows = q_rows[token_rows, group * BANK:(group + 1) * BANK]
             nc.sync.dma_start(out=rows.rearrange("(j p) c -> p j c", p=P), in_=result)
 
+        def reciprocal_root(n, heads):
+            nc.scalar.activation(
+                out=rstd[:, n, heads], in_=sum_squares[:, n, heads], func=ACT.Abs_reciprocal_sqrt,
+                bias=eps[:, 0:1], scale=1.0 / HEAD,
+            )
+
         def finish_waiting_bank():
             for acc, n, m, group in waiting:
-                nc.scalar.activation(
-                    out=rstd[:, n, :], in_=sum_squares[:, n, :], func=ACT.Abs_reciprocal_sqrt,
-                    bias=eps[:, 0:1], scale=1.0 / HEAD,
-                )
+                if n > 0:
+                    reciprocal_root(n, slice(0, HEADS_PER_BANK))
                 a = m % TILES_PER_BATCH
                 table = table_k if group == K_GROUP else table_q
                 paired = SINGLE_FIRST <= n < ROPE_BANKS - SINGLE_LAST
                 j = m % 2 if paired else 0
                 if not paired:
                     products = work.tile([P, 1, HEADS_PER_BANK, 2, HEAD], F32, tag="products1", bufs=3)
-                    result = results.tile([P, 1, BANK], F32, tag="result1", bufs=4)
+                    result = results.tile([P, 1, BANK], F32, tag="result1", bufs=8)
                     open_batch.append((products, result))
                 elif j == 0:
                     products = work.tile([P, 2, HEADS_PER_BANK, 2, HEAD], F32, tag="products2", bufs=3)
-                    result = results.tile([P, 2, BANK], F32, tag="result2", bufs=4)
+                    result = results.tile([P, 2, BANK], F32, tag="result2", bufs=6)
                     open_batch.append((products, result))
                 products, result = open_batch[0]
                 for h in range(HEADS_PER_BANK):
@@ -326,6 +337,10 @@ def tile_attention_pa_kernel(
             finish_waiting_bank()
             for h in range(1, HEADS_PER_BANK):
                 square(acc, n, h)
+                if n == 0:
+                    reciprocal_root(n, slice(h - 1, h))
+            if n == 0:
+                reciprocal_root(n, slice(HEADS_PER_BANK - 1, HEADS_PER_BANK))
             waiting.append((acc, n, m, group))
             if n < ROOT_AT_ONCE:
                 finish_waiting_bank()
@@ -359,10 +374,9 @@ def tile_attention_pa_kernel(
             op0=ALU.mult, op1=ALU.add,
         )
         quantise_token_tile(1)
-        transpose_token_tile(2, ("scalar", "vector"))
+        transpose_token_tile(2, ("scalar", "scalar"))
         quantise_token_tile(2)
         transpose_token_tile(3, ("scalar", "scalar"))
-        keep_clock_up(WARM_BETWEEN)
         quantise_token_tile(3)
 
         for group in range(V_GROUP):

@@ -32,7 +32,7 @@ ROPE_BANKS = TOKEN_TILES * V_GROUP
 EPS = 1e-6
 ROPE_THETA = 10000.0
 SQUARE_SLICES = 8
-SINGLE_FIRST = 6
+SINGLE_FIRST = 8
 SINGLE_LAST = 2
 ROOT_AT_ONCE = 2
 WARM_BEFORE_X = 4
@@ -186,11 +186,13 @@ def tile_attention_pa_kernel(
                 in1=turn[:, a, :], op0=ALU.subtract, op1=ALU.subtract,
             )
         trig = keep.tile([P, TILES_PER_BATCH * 2, HEAD], F32)
-        nc.scalar.activation(
-            out=trig[:].rearrange("p c j -> p (c j)"),
-            in_=whole_less_turn[:].rearrange("p a c -> p (a c)"), func=ACT.Sin,
-            scale=-2.0 * math.pi,
-        )
+
+        def sines():
+            nc.scalar.activation(
+                out=trig[:].rearrange("p c j -> p (c j)"),
+                in_=whole_less_turn[:].rearrange("p a c -> p (a c)"), func=ACT.Sin,
+                scale=-2.0 * math.pi,
+            )
 
         def keep_clock_up(count):
             unread = psum.tile([P, BANK], F32, tag="bank")
@@ -227,12 +229,15 @@ def tile_attention_pa_kernel(
                 else:
                     nc.vector.tensor_copy(out=destination, in_=source)
 
-        def quantise_token_tile(m):
-            nc.vector.quantize_mx(
-                out=x_codes[m][:].rearrange("p g r -> p (g r)").bitcast(FP8X4),
-                scales=x_scales[m][:].rearrange("p g r -> p (g r)"),
-                in_=grouped_tiles[m][:].rearrange("p g r t -> p (g r t)"),
-            )
+        def quantise_token_tile(m, pieces=1):
+            passes = PASSES // pieces
+            for piece in range(pieces):
+                some = slice(piece * passes, (piece + 1) * passes)
+                nc.vector.quantize_mx(
+                    out=x_codes[m][:, some, :].rearrange("p g r -> p (g r)").bitcast(FP8X4),
+                    scales=x_scales[m][:, some, :].rearrange("p g r -> p (g r)"),
+                    in_=grouped_tiles[m][:, some, :, :].rearrange("p g r t -> p (g r t)"),
+                )
 
         def project(m, group):
             acc = psum.tile([P, BANK], F32, tag="bank")
@@ -301,11 +306,11 @@ def tile_attention_pa_kernel(
                 j = m % 2 if paired else 0
                 if not paired:
                     products = work.tile([P, 1, HEADS_PER_BANK, 2, HEAD], F32, tag="products1", bufs=3)
-                    result = results.tile([P, 1, BANK], F32, tag="result1", bufs=8)
+                    result = results.tile([P, 1, BANK], F32, tag="result1", bufs=10)
                     open_batch.append((products, result))
                 elif j == 0:
                     products = work.tile([P, 2, HEADS_PER_BANK, 2, HEAD], F32, tag="products2", bufs=3)
-                    result = results.tile([P, 2, BANK], F32, tag="result2", bufs=6)
+                    result = results.tile([P, 2, BANK], F32, tag="result2", bufs=5)
                     open_batch.append((products, result))
                 products, result = open_batch[0]
                 for h in range(HEADS_PER_BANK):
@@ -346,10 +351,11 @@ def tile_attention_pa_kernel(
                 finish_waiting_bank()
 
         keep_clock_up(WARM_BEFORE_X)
-        transpose_token_tile(0, ("scalar", "vector"))
-        quantise_token_tile(0)
+        transpose_token_tile(0, ("scalar", "scalar"))
+        sines()
         nc.scalar.activation(out=warm[:], in_=eps[:], func=ACT.Abs_reciprocal_sqrt)
-        transpose_token_tile(1, ("scalar", "vector"))
+        quantise_token_tile(0)
+        transpose_token_tile(1, ("vector", "vector"))
         keep_clock_up(WARM_BETWEEN)
 
         spread = psum.tile([P, BANK], F32, tag="bank")
@@ -367,17 +373,17 @@ def tile_attention_pa_kernel(
             return table
 
         table_q = rope_table(spread[:, 0:HEAD], "table_q")
+        quantise_token_tile(1)
         table_k = rope_table(spread[:, HEAD:2 * HEAD], "table_k")
         one_minus_lambda = keep.tile([P, 1], F32)
         nc.vector.tensor_scalar(
             out=one_minus_lambda[:], in0=spread[:, 2 * HEAD:2 * HEAD + 1], scalar1=-1.0, scalar2=1.0,
             op0=ALU.mult, op1=ALU.add,
         )
-        quantise_token_tile(1)
         transpose_token_tile(2, ("scalar", "scalar"))
         quantise_token_tile(2)
         transpose_token_tile(3, ("scalar", "scalar"))
-        quantise_token_tile(3)
+        quantise_token_tile(3, 2)
 
         for group in range(V_GROUP):
             for m in range(TOKEN_TILES):

@@ -34,7 +34,6 @@ ROPE_THETA = 10000.0
 SQUARE_SLICES = 8
 SINGLE_FIRST = 8
 SINGLE_LAST = 2
-ROOT_AT_ONCE = 2
 WARM_BEFORE_X = 4
 WARM_BETWEEN = 2
 SMALL_COLUMNS = 2 * HEAD + 2
@@ -263,6 +262,27 @@ def tile_attention_pa_kernel(
             )
             nc.scalar.dma_start(out=v_rows[m * P:(m + 1) * P, :], in_=result[:])
 
+        def value_bank_by_heads(m):
+            result = results.tile([P, BANK], F32, tag="value_result", bufs=TOKEN_TILES)
+            for h in range(HEADS_PER_BANK):
+                columns = slice(h * HEAD, (h + 1) * HEAD)
+                acc = psum.tile([P, BANK], F32, tag="bank")
+                for g in range(PASSES):
+                    nc.tensor.matmul_mx(
+                        out=acc[:, 0:HEAD],
+                        lhsT=x_codes[m][:, g, :].bitcast(FP8X4),
+                        lhsT_scale=x_scales[m][:, g, :],
+                        rhs=w_words[V_GROUP][:, g, 2 * HEAD * h:2 * HEAD * (h + 1)].bitcast(FP4X4),
+                        rhs_scale=w_planes[V_GROUP // 2][:, g, BANK + HEAD * h:BANK + HEAD * (h + 1)],
+                        start=(g == 0),
+                        stop=(g == PASSES - 1),
+                    )
+                nc.vector.scalar_tensor_tensor(
+                    out=result[:, columns], in0=v1_sb[:, m, columns], scalar=one_minus_lambda[:, 0:1],
+                    in1=acc[:, 0:HEAD], op0=ALU.mult, op1=ALU.add,
+                )
+                nc.scalar.dma_start(out=v_rows[m * P:(m + 1) * P, columns], in_=result[:, columns])
+
         squares_written = []
         waiting = []
 
@@ -296,31 +316,39 @@ def tile_attention_pa_kernel(
                 bias=eps[:, 0:1], scale=1.0 / HEAD,
             )
 
+        def rope_products(acc, n, m, group, products, j, heads):
+            a = m % TILES_PER_BATCH
+            table = table_k if group == K_GROUP else table_q
+            for h in heads:
+                nc.vector.scalar_tensor_tensor(
+                    out=products[:, j, h, :, :],
+                    in0=table[:, 2 * a:2 * a + 2, :],
+                    scalar=rstd[:, n, h:h + 1],
+                    in1=acc[:, h * HEAD:(h + 1) * HEAD].unsqueeze(1).to_broadcast([P, 2, HEAD]),
+                    op0=ALU.mult, op1=ALU.mult,
+                )
+
+        def begin_epilogue(acc, n, m, group):
+            reciprocal_root(n, slice(0, HEADS_PER_BANK - 1))
+            paired = SINGLE_FIRST <= n < ROPE_BANKS - SINGLE_LAST
+            j = m % 2 if paired else 0
+            if not paired:
+                products = work.tile([P, 1, HEADS_PER_BANK, 2, HEAD], F32, tag="products1", bufs=3)
+                result = results.tile([P, 1, BANK], F32, tag="result1", bufs=10)
+                open_batch.append((products, result))
+            elif j == 0:
+                products = work.tile([P, 2, HEADS_PER_BANK, 2, HEAD], F32, tag="products2", bufs=3)
+                result = results.tile([P, 2, BANK], F32, tag="result2", bufs=5)
+                open_batch.append((products, result))
+            products, result = open_batch[0]
+            rope_products(acc, n, m, group, products, j, range(HEADS_PER_BANK - 1))
+            waiting.append((acc, n, m, group, paired, j))
+
         def finish_waiting_bank():
-            for acc, n, m, group in waiting:
-                if n > 0:
-                    reciprocal_root(n, slice(0, HEADS_PER_BANK))
-                a = m % TILES_PER_BATCH
-                table = table_k if group == K_GROUP else table_q
-                paired = SINGLE_FIRST <= n < ROPE_BANKS - SINGLE_LAST
-                j = m % 2 if paired else 0
-                if not paired:
-                    products = work.tile([P, 1, HEADS_PER_BANK, 2, HEAD], F32, tag="products1", bufs=3)
-                    result = results.tile([P, 1, BANK], F32, tag="result1", bufs=10)
-                    open_batch.append((products, result))
-                elif j == 0:
-                    products = work.tile([P, 2, HEADS_PER_BANK, 2, HEAD], F32, tag="products2", bufs=3)
-                    result = results.tile([P, 2, BANK], F32, tag="result2", bufs=5)
-                    open_batch.append((products, result))
+            for acc, n, m, group, paired, j in waiting:
+                reciprocal_root(n, slice(HEADS_PER_BANK - 1, HEADS_PER_BANK))
                 products, result = open_batch[0]
-                for h in range(HEADS_PER_BANK):
-                    nc.vector.scalar_tensor_tensor(
-                        out=products[:, j, h, :, :],
-                        in0=table[:, 2 * a:2 * a + 2, :],
-                        scalar=rstd[:, n, h:h + 1],
-                        in1=acc[:, h * HEAD:(h + 1) * HEAD].unsqueeze(1).to_broadcast([P, 2, HEAD]),
-                        op0=ALU.mult, op1=ALU.mult,
-                    )
+                rope_products(acc, n, m, group, products, j, range(HEADS_PER_BANK - 1, HEADS_PER_BANK))
                 if n == ROPE_BANKS - 1:
                     left_for_vector.append((products, result, m, group))
                     open_batch.clear()
@@ -342,12 +370,8 @@ def tile_attention_pa_kernel(
             finish_waiting_bank()
             for h in range(1, HEADS_PER_BANK):
                 square(acc, n, h)
-                if n == 0:
-                    reciprocal_root(n, slice(h - 1, h))
+            begin_epilogue(acc, n, m, group)
             if n == 0:
-                reciprocal_root(n, slice(HEADS_PER_BANK - 1, HEADS_PER_BANK))
-            waiting.append((acc, n, m, group))
-            if n < ROOT_AT_ONCE:
                 finish_waiting_bank()
 
         keep_clock_up(WARM_BEFORE_X)
@@ -389,7 +413,8 @@ def tile_attention_pa_kernel(
             for m in range(TOKEN_TILES):
                 rope_bank(m, group)
         finish_waiting_bank()
-        for m in range(TOKEN_TILES):
+        for m in range(TOKEN_TILES - 1):
             value_bank(m)
+        value_bank_by_heads(TOKEN_TILES - 1)
         for products, result, m, group in left_for_vector:
             add_and_store(nc.vector, products[:], result[:], m, 1, group)

@@ -32,8 +32,8 @@ ROPE_BANKS = TOKEN_TILES * V_GROUP
 EPS = 1e-6
 ROPE_THETA = 10000.0
 SQUARE_SLICES = 8
-SINGLE_FIRST = 8
-SINGLE_LAST = 2
+SINGLE_FIRST = 6
+SINGLE_LAST = 4
 WARM_BEFORE_X = 4
 WARM_BETWEEN = 2
 SMALL_COLUMNS = 2 * HEAD + 2
@@ -333,7 +333,7 @@ def tile_attention_pa_kernel(
             paired = SINGLE_FIRST <= n < ROPE_BANKS - SINGLE_LAST
             j = m % 2 if paired else 0
             if not paired:
-                products = work.tile([P, 1, HEADS_PER_BANK, 2, HEAD], F32, tag="products1", bufs=3)
+                products = work.tile([P, 1, HEADS_PER_BANK, 2, HEAD], F32, tag="products1", bufs=4)
                 result = results.tile([P, 1, BANK], F32, tag="result1", bufs=10)
                 open_batch.append((products, result))
             elif j == 0:

@@ -150,14 +150,17 @@ def tile_attention_pa_kernel(
         load_scales(0, Wq_scales, 0)
         load_words_by_pass(0, Wq_words, 0)
         load_words(1, Wq_words, BANK)
-        for c in (1, 2):
+        def write_every_row(c):
             nc.sync.dma_start(
                 out=w_planes[c][:].rearrange("p g n -> p (g n)").bitcast(I32),
                 in_=Wq_words.bitcast(I32)[0, :, :],
             )
+
+        write_every_row(1)
         load_words(2, Wq_words, 2 * BANK)
         load_words(3, Wq_words, 3 * BANK)
         load_scales(1, Wq_scales, CHUNK)
+        write_every_row(2)
         load_words(K_GROUP, Wkv_words, 0)
         load_words(V_GROUP, Wkv_words, BANK)
         load_scales(2, Wkv_scales, 0)

@@ -149,7 +149,6 @@ def tile_attention_pa_kernel(
         nc.vector.memset(w_planes[0][:].bitcast(I32), 0)
         load_scales(0, Wq_scales, 0)
         load_words_by_pass(0, Wq_words, 0)
-        load_words(1, Wq_words, BANK)
         def write_every_row(c):
             nc.sync.dma_start(
                 out=w_planes[c][:].rearrange("p g n -> p (g n)").bitcast(I32),
@@ -157,9 +156,10 @@ def tile_attention_pa_kernel(
             )
 
         write_every_row(1)
+        load_words(1, Wq_words, BANK)
         load_words(2, Wq_words, 2 * BANK)
-        load_words(3, Wq_words, 3 * BANK)
         load_scales(1, Wq_scales, CHUNK)
+        load_words(3, Wq_words, 3 * BANK)
         write_every_row(2)
         load_words(K_GROUP, Wkv_words, 0)
         load_words(V_GROUP, Wkv_words, BANK)

import math

import concourse.mybir as mybir
from concourse.masks import make_identity

F32 = mybir.dt.float32
BF16 = mybir.dt.bfloat16
I32 = mybir.dt.int32
U32 = mybir.dt.uint32
U8 = mybir.dt.uint8
FP8X4 = mybir.dt.float8_e4m3fn_x4
FP4X4 = mybir.dt.float4_e2m1fn_x4
ALU = mybir.AluOpType
ACT = mybir.ActivationFunctionType

P = 128
BATCH, T, C = 2, 256, 2048
HEAD = 128
HALF = HEAD // 2
FREQ_LEVELS = 3
K_PASS = 512
PASSES = C // K_PASS
BANK = 512
PSUM_BANKS = 8
HEADS_PER_BANK = BANK // HEAD
TILES_PER_BATCH = T // P
TOKEN_TILES = BATCH * TILES_PER_BATCH
CHUNK = 2 * BANK
GROUPS = 6
K_GROUP, V_GROUP = 4, 5
ROPE_BANKS = TOKEN_TILES * V_GROUP
EPS = 1e-6
ROPE_THETA = 10000.0
SQUARE_SLICES = 8
SINGLE_FIRST = 6
SINGLE_LAST = 4
WARM_BEFORE_X = 4
WARM_BETWEEN = 2
SMALL_COLUMNS = 2 * HEAD + 2
ROUND_MAGIC = 1.5 * 2.0**23

FLOPS = 2 * BATCH * T * C * GROUPS * BANK


def tile_attention_pa_kernel(
    tc, x, Wq_words, Wq_scales, Wkv_words, Wkv_scales, q_scale, k_scale, v1, value_lambda,
    out_0, out_1, out_2,
):
    nc = tc.nc
    x_rows = x.flatten_outer_dims()
    v1_rows = v1.rearrange("b t h d -> (b t) (h d)")
    q_rows = out_0.rearrange("b t h d -> (b t) (h d)")
    k_rows = out_1.rearrange("b t h d -> (b t) (h d)")
    v_rows = out_2.rearrange("b t h d -> (b t) (h d)")

    with tc.tile_pool(name="keep", bufs=1) as keep, \
            tc.tile_pool(name="stage", bufs=TOKEN_TILES) as stage, \
            tc.tile_pool(name="work", bufs=3) as work, \
            tc.tile_pool(name="results", bufs=4) as results, \
            tc.psum_pool(name="psum", bufs=PSUM_BANKS) as psum, \
            tc.manual_schedule():

        x_sb = [keep.tile([P, C], BF16, name="x_sb%d" % m) for m in range(TOKEN_TILES)]
        x_codes = [
            keep.tile([P, PASSES, P], U32, name="x_codes%d" % m, align_bytes=64)
            for m in range(TOKEN_TILES)
        ]
        x_scales = [
            keep.tile([P, PASSES, P], U8, name="x_scales%d" % m, align_bytes=64)
            for m in range(TOKEN_TILES)
        ]
        w_words = [
            keep.tile([P, PASSES, 2 * BANK], U8, name="w_words%d" % group, align_bytes=64)
            for group in range(GROUPS)
        ]
        w_planes = [
            keep.tile([P, PASSES, CHUNK], U8, name="w_planes%d" % c, align_bytes=64)
            for c in range(GROUPS // 2)
        ]
        v1_sb = keep.tile([P, TOKEN_TILES, BANK], BF16)
        small_row = keep.tile([P, SMALL_COLUMNS], BF16)
        ones = keep.tile([P, BANK], BF16)
        identity = keep.tile([P, P], F32)
        eps = keep.tile([P, 1], F32)
        warm = keep.tile([P, 1], F32)
        squares = keep.tile([P, SQUARE_SLICES, HEAD], F32)
        sum_squares = keep.tile([P, ROPE_BANKS, HEADS_PER_BANK], F32)
        rstd = keep.tile([P, ROPE_BANKS, HEADS_PER_BANK], F32)

        def load_x(m, pieces=1):
            width = C // pieces
            for piece in range(pieces):
                columns = slice(piece * width, (piece + 1) * width)
                nc.sync.dma_start(out=x_sb[m][:, columns], in_=x_rows[m * P:(m + 1) * P, columns])

        def load_scales(c, scales, first_column):
            scale_words = scales.bitcast(I32)[:, :, first_column // 4:(first_column + CHUNK) // 4]
            for row in range(4):
                nc.sync.dma_start(
                    out=w_planes[c][row:P:32, :, :].bitcast(I32),
                    in_=scale_words[:, row:16:4, :].rearrange("g q w -> q g w"),
                )

        def load_words(group, words, first_column):
            nc.sync.dma_start(
                out=w_words[group][:].bitcast(I32),
                in_=words.bitcast(I32)[:, :, first_column // 2:(first_column + BANK) // 2]
                .rearrange("g p w -> p g w"),
            )

        def load_words_by_pass(group, words, first_column):
            for g in range(PASSES):
                nc.sync.dma_start(
                    out=w_words[group][:, g, :].bitcast(I32),
                    in_=words.bitcast(I32)[g, :, first_column // 2:(first_column + BANK) // 2],
                )

        nc.vector.memset(eps[:], EPS)
        nc.vector.memset(ones[:], 1.0)
        position_i = keep.tile([P, TILES_PER_BATCH], I32)
        nc.gpsimd.iota(position_i[:], pattern=[[P, TILES_PER_BATCH]], base=0, channel_multiplier=1)
        make_identity(nc, identity[:])
        nc.scalar.activation(out=warm[:], in_=eps[:], func=ACT.Sin)
        load_x(0, 2)
        load_x(1)
        load_x(2)
        load_x(3, 2)

        freq = keep.tile([P, 4, HALF], F32)
        nc.vector.memset(freq[:, :, 0:1], 1.0)
        nc.vector.memset(freq[:, 1:2, 0:1], -1.0)

        def freq_level(level):
            width = 4 ** level
            for j in range(1, 4):
                nc.vector.tensor_scalar_mul(
                    out=freq[:, :, j * width:(j + 1) * width], in0=freq[:, :, 0:width],
                    scalar1=ROPE_THETA ** (-(j * width) / HALF),
                )

        freq_level(0)
        nc.vector.memset(small_row[:], 0.0)
        nc.scalar.dma_start(out=small_row[0:1, 0:HEAD], in_=q_scale.rearrange("(o n) -> o n", o=1))
        nc.scalar.dma_start(out=small_row[0:1, HEAD:2 * HEAD], in_=k_scale.rearrange("(o n) -> o n", o=1))
        nc.scalar.dma_start(
            out=small_row[0:1, 2 * HEAD:2 * HEAD + 1], in_=value_lambda.rearrange("(o n) -> o n", o=1)
        )
        freq_level(1)
        nc.vector.memset(w_planes[0][:].bitcast(I32), 0)
        load_scales(0, Wq_scales, 0)
        load_words_by_pass(0, Wq_words, 0)
        def write_every_row(c):
            nc.sync.dma_start(
                out=w_planes[c][:].rearrange("p g n -> p (g n)").bitcast(I32),
                in_=Wq_words.bitcast(I32)[0, :, :],
            )

        write_every_row(1)
        load_words(1, Wq_words, BANK)
        load_words(2, Wq_words, 2 * BANK)
        load_scales(1, Wq_scales, CHUNK)
        load_words(3, Wq_words, 3 * BANK)
        write_every_row(2)
        load_words(K_GROUP, Wkv_words, 0)
        load_words(V_GROUP, Wkv_words, BANK)
        load_scales(2, Wkv_scales, 0)
        nc.sync.dma_start(out=v1_sb[:], in_=v1_rows.rearrange("(m p) c -> p m c", p=P))
        freq_level(2)
        position_turns = keep.tile([P, TILES_PER_BATCH], F32)
        nc.vector.tensor_scalar_mul(out=position_turns[:], in0=position_i[:], scalar1=1.0 / (2.0 * math.pi))
        turn = keep.tile([P, TILES_PER_BATCH, 4 * HALF], F32)
        for a in range(TILES_PER_BATCH):
            blocks = turn[:, a, :].rearrange("p (b i) -> p b i", i=HALF)
            nc.vector.tensor_scalar(
                out=blocks[:, 0:4:3, :], in0=freq[:, 0:4:3, :], scalar1=position_turns[:, a:a + 1],
                scalar2=0.25, op0=ALU.mult, op1=ALU.add,
            )
            nc.vector.tensor_scalar_mul(
                out=blocks[:, 1:3, :], in0=freq[:, 1:3, :], scalar1=position_turns[:, a:a + 1]
            )
        shifted = keep.tile([P, TILES_PER_BATCH, 4 * HALF], F32)
        whole_less_turn = keep.tile([P, TILES_PER_BATCH, 4 * HALF], F32)
        for a in range(TILES_PER_BATCH):
            nc.vector.tensor_scalar_add(out=shifted[:, a, :], in0=turn[:, a, :], scalar1=ROUND_MAGIC)
        for a in range(TILES_PER_BATCH):
            nc.vector.scalar_tensor_tensor(
                out=whole_less_turn[:, a, :], in0=shifted[:, a, :], scalar=ROUND_MAGIC,
                in1=turn[:, a, :], op0=ALU.subtract, op1=ALU.subtract,
            )
        trig = keep.tile([P, TILES_PER_BATCH * 2, HEAD], F32)

        def sines():
            nc.scalar.activation(
                out=trig[:].rearrange("p c j -> p (c j)"),
                in_=whole_less_turn[:].rearrange("p a c -> p (a c)"), func=ACT.Sin,
                scale=-2.0 * math.pi,
            )

        def keep_clock_up(count):
            unread = psum.tile([P, BANK], F32, tag="bank")
            for repeat in range(count):
                nc.tensor.matmul(
                    out=unread[:], lhsT=ones[:, 0:P], rhs=ones[:],
                    start=(repeat == 0), stop=(repeat == count - 1),
                )

        grouped_tiles = {}

        def transpose_token_tile(m, copy_engines):
            x_words = x_sb[m][:].bitcast(F32)
            grouped = stage.tile([P, PASSES, P, 4], BF16, align_bytes=64)
            grouped_tiles[m] = grouped
            grouped_words = grouped[:].bitcast(F32)
            banks = []
            for pair in range(PASSES // 2):
                turned = psum.tile([P, 2, 2, P], F32, tag="bank")
                for j in range(2):
                    first_word = (K_PASS // 2) * (2 * pair + j)
                    for u in range(2):
                        nc.tensor.transpose(
                            turned[:, j, u, :],
                            x_words[:, first_word + u:first_word + K_PASS // 2:2],
                            identity[:],
                        )
                banks.append(turned)
            for pair in range(PASSES // 2):
                destination = grouped_words[:, 2 * pair:2 * pair + 2, :, :]
                source = banks[pair][:].rearrange("p j u r -> p j r u")
                if copy_engines[pair] == "scalar":
                    nc.scalar.copy(out=destination, in_=source)
                else:
                    nc.vector.tensor_copy(out=destination, in_=source)

        def quantise_token_tile(m, pieces=1):
            passes = PASSES // pieces
            for piece in range(pieces):
                some = slice(piece * passes, (piece + 1) * passes)
                nc.vector.quantize_mx(
                    out=x_codes[m][:, some, :].rearrange("p g r -> p (g r)").bitcast(FP8X4),
                    scales=x_scales[m][:, some, :].rearrange("p g r -> p (g r)"),
                    in_=grouped_tiles[m][:, some, :, :].rearrange("p g r t -> p (g r t)"),
                )

        def project(m, group):
            acc = psum.tile([P, BANK], F32, tag="bank")
            half = group % 2
            for g in range(PASSES):
                nc.tensor.matmul_mx(
                    out=acc[:],
                    lhsT=x_codes[m][:, g, :].bitcast(FP8X4),
                    lhsT_scale=x_scales[m][:, g, :],
                    rhs=w_words[group][:, g, :].bitcast(FP4X4),
                    rhs_scale=w_planes[group // 2][:, g, BANK * half:BANK * (half + 1)],
                    start=(g == 0),
                    stop=(g == PASSES - 1),
                )
            return acc

        def value_bank(m):
            acc = project(m, V_GROUP)
            result = results.tile([P, BANK], F32, tag="value_result", bufs=TOKEN_TILES)
            nc.vector.scalar_tensor_tensor(
                out=result[:], in0=v1_sb[:, m, :], scalar=one_minus_lambda[:, 0:1],
                in1=acc[:], op0=ALU.mult, op1=ALU.add,
            )
            nc.scalar.dma_start(out=v_rows[m * P:(m + 1) * P, :], in_=result[:])

        def value_bank_by_heads(m):
            result = results.tile([P, BANK], F32, tag="value_result", bufs=TOKEN_TILES)
            for h in range(HEADS_PER_BANK):
                columns = slice(h * HEAD, (h + 1) * HEAD)
                acc = psum.tile([P, BANK], F32, tag="bank")
                for g in range(PASSES):
                    nc.tensor.matmul_mx(
                        out=acc[:, 0:HEAD],
                        lhsT=x_codes[m][:, g, :].bitcast(FP8X4),
                        lhsT_scale=x_scales[m][:, g, :],
                        rhs=w_words[V_GROUP][:, g, 2 * HEAD * h:2 * HEAD * (h + 1)].bitcast(FP4X4),
                        rhs_scale=w_planes[V_GROUP // 2][:, g, BANK + HEAD * h:BANK + HEAD * (h + 1)],
                        start=(g == 0),
                        stop=(g == PASSES - 1),
                    )
                nc.vector.scalar_tensor_tensor(
                    out=result[:, columns], in0=v1_sb[:, m, columns], scalar=one_minus_lambda[:, 0:1],
                    in1=acc[:, 0:HEAD], op0=ALU.mult, op1=ALU.add,
                )
                nc.scalar.dma_start(out=v_rows[m * P:(m + 1) * P, columns], in_=result[:, columns])

        squares_written = []
        waiting = []

        def square(acc, n, h):
            nc.scalar.activation(
                out=squares[:, len(squares_written) % SQUARE_SLICES, :],
                in_=acc[:, h * HEAD:(h + 1) * HEAD], func=ACT.Square,
                accum_out=sum_squares[:, n, h:h + 1],
            )
            squares_written.append(h)

        left_for_vector = []
        open_batch = []

        def add_and_store(engine, products, result, first_tile, tiles, group):
            terms = products.rearrange("p j h o (s i) -> p (j h o) s i", s=2)
            engine.tensor_tensor(
                out=result.rearrange("p j (c i) -> p (j c) i", i=HALF),
                in0=terms[:, :, 0, :], in1=terms[:, :, 1, :], op=ALU.add,
            )
            token_rows = slice(first_tile * P, (first_tile + tiles) * P)
            if group == K_GROUP:
                rows = k_rows[token_rows, :]
            else:
                rows = q_rows[token_rows, group * BANK:(group + 1) * BANK]
            nc.sync.dma_start(out=rows.rearrange("(j p) c -> p j c", p=P), in_=result)

        def reciprocal_root(n, heads):
            nc.scalar.activation(
                out=rstd[:, n, heads], in_=sum_squares[:, n, heads], func=ACT.Abs_reciprocal_sqrt,
                bias=eps[:, 0:1], scale=1.0 / HEAD,
            )

        def rope_products(acc, n, m, group, products, j, heads):
            a = m % TILES_PER_BATCH
            table = table_k if group == K_GROUP else table_q
            for h in heads:
                nc.vector.scalar_tensor_tensor(
                    out=products[:, j, h, :, :],
                    in0=table[:, 2 * a:2 * a + 2, :],
                    scalar=rstd[:, n, h:h + 1],
                    in1=acc[:, h * HEAD:(h + 1) * HEAD].unsqueeze(1).to_broadcast([P, 2, HEAD]),
                    op0=ALU.mult, op1=ALU.mult,
                )

        def begin_epilogue(acc, n, m, group):
            reciprocal_root(n, slice(0, HEADS_PER_BANK - 1))
            paired = SINGLE_FIRST <= n < ROPE_BANKS - SINGLE_LAST
            j = m % 2 if paired else 0
            if not paired:
                products = work.tile([P, 1, HEADS_PER_BANK, 2, HEAD], F32, tag="products1", bufs=4)
                result = results.tile([P, 1, BANK], F32, tag="result1", bufs=10)
                open_batch.append((products, result))
            elif j == 0:
                products = work.tile([P, 2, HEADS_PER_BANK, 2, HEAD], F32, tag="products2", bufs=3)
                result = results.tile([P, 2, BANK], F32, tag="result2", bufs=5)
                open_batch.append((products, result))
            products, result = open_batch[0]
            rope_products(acc, n, m, group, products, j, range(HEADS_PER_BANK - 1))
            waiting.append((acc, n, m, group, paired, j))

        def finish_waiting_bank():
            for acc, n, m, group, paired, j in waiting:
                reciprocal_root(n, slice(HEADS_PER_BANK - 1, HEADS_PER_BANK))
                products, result = open_batch[0]
                rope_products(acc, n, m, group, products, j, range(HEADS_PER_BANK - 1, HEADS_PER_BANK))
                if n == ROPE_BANKS - 1:
                    left_for_vector.append((products, result, m, group))
                    open_batch.clear()
                elif not paired:
                    add_and_store(nc.gpsimd, products[:], result[:], m, 1, group)
                    open_batch.clear()
                elif j == 1:
                    add_and_store(nc.gpsimd, products[:], result[:], m - 1, 2, group)
                    open_batch.clear()
            waiting.clear()

        rope_banks_begun = []

        def rope_bank(m, group):
            n = len(rope_banks_begun)
            rope_banks_begun.append(n)
            acc = project(m, group)
            square(acc, n, 0)
            finish_waiting_bank()
            for h in range(1, HEADS_PER_BANK):
                square(acc, n, h)
            begin_epilogue(acc, n, m, group)
            if n == 0:
                finish_waiting_bank()

        keep_clock_up(WARM_BEFORE_X)
        transpose_token_tile(0, ("scalar", "scalar"))
        sines()
        nc.scalar.activation(out=warm[:], in_=eps[:], func=ACT.Abs_reciprocal_sqrt)
        quantise_token_tile(0)
        transpose_token_tile(1, ("vector", "vector"))
        keep_clock_up(WARM_BETWEEN)

        spread = psum.tile([P, BANK], F32, tag="bank")
        nc.tensor.matmul(
            out=spread[:, 0:SMALL_COLUMNS], lhsT=ones[:, 0:P], rhs=small_row[:], start=True, stop=True
        )

        def rope_table(gain, name):
            table = keep.tile([P, TILES_PER_BATCH * 2, HEAD], F32, name=name)
            nc.vector.tensor_tensor(
                out=table[:], in0=trig[:],
                in1=gain.unsqueeze(1).to_broadcast([P, TILES_PER_BATCH * 2, HEAD]),
                op=ALU.mult,
            )
            return table

        table_q = rope_table(spread[:, 0:HEAD], "table_q")
        quantise_token_tile(1)
        table_k = rope_table(spread[:, HEAD:2 * HEAD], "table_k")
        one_minus_lambda = keep.tile([P, 1], F32)
        nc.vector.tensor_scalar(
            out=one_minus_lambda[:], in0=spread[:, 2 * HEAD:2 * HEAD + 1], scalar1=-1.0, scalar2=1.0,
            op0=ALU.mult, op1=ALU.add,
        )
        transpose_token_tile(2, ("scalar", "scalar"))
        quantise_token_tile(2)
        transpose_token_tile(3, ("scalar", "scalar"))
        quantise_token_tile(3, 2)

        for group in range(V_GROUP):
            for m in range(TOKEN_TILES):
                rope_bank(m, group)
        finish_waiting_bank()
        for m in range(TOKEN_TILES - 1):
            value_bank(m)
        value_bank_by_heads(TOKEN_TILES - 1)
        for products, result, m, group in left_for_vector:
            add_and_store(nc.vector, products[:], result[:], m, 1, group)
